import numpy as np
import ml_dtypes


def mxq(x, axis, fmt="e4m3"):
    dtype, down = {"e4m3": (ml_dtypes.float8_e4m3fn, 7), "e5m2": (ml_dtypes.float8_e5m2, 14)}[fmt]
    v = np.moveaxis(np.asarray(x, np.float32).astype(ml_dtypes.bfloat16).astype(np.float64), axis, -1)
    blocks = v.reshape(v.shape[:-1] + (-1, 32))
    amax = np.abs(blocks).max(-1, keepdims=True)
    byte = np.maximum(np.where(amax > 0, np.frexp(amax)[1] - 1 + 127, 0) - down, 1)
    scale = np.exp2(byte - 127.0)
    codes = (blocks / scale).astype(np.float32).astype(dtype).astype(np.float64)
    return np.moveaxis((codes * scale).reshape(v.shape), -1, axis)


WIDE = False


def mx_kscale(k):
    if not WIDE:
        return np.ones(k)
    levels = np.array([10, -10, 5, -5, 0])
    a = np.random.permutation(np.resize(levels, k // 512 * 4)).reshape(k // 512, 4)
    idx = np.arange(k)
    return np.exp2(a[idx // 512, idx % 128 // 32])


BF16 = ml_dtypes.bfloat16


def bf(x):
    return np.asarray(x, np.float32).astype(BF16)


def f64(x):
    return np.asarray(x).astype(np.float64)


E2M1 = np.array([0.0, 0.5, 1.0, 1.5, 2.0, 3.0, 4.0, 6.0, -0.0, -0.5, -1.0, -1.5, -2.0, -3.0, -4.0, -6.0])


def pack_weight(w, fmt):
    k, n = w.shape
    w = f64(bf(w)).reshape(k // 32, 32, n)
    amax = np.abs(w).max(1)
    if fmt == "e4m3":
        byte = np.frexp(amax)[1] - 1 + 127 - 7
    else:
        mant, ex = np.frexp(amax / 6.0)
        byte = np.where(mant > 0.5, ex, ex - 1) + 127
    byte = np.clip(np.where(amax > 0, byte, 1), 1, 254)
    scaled = (w * np.exp2(127.0 - byte)[:, None, :]).reshape(k, n).astype(np.float32)
    by_word = np.ascontiguousarray(scaled.reshape(k // 512, 128, 4, n).transpose(0, 1, 3, 2))
    if fmt == "e4m3":
        words = by_word.astype(ml_dtypes.float8_e4m3fn).view(np.uint8)
    else:
        c = by_word.astype(ml_dtypes.float4_e2m1fn).view(np.uint8) & 0xF
        words = c[..., 0::2] | (c[..., 1::2] << 4)
    return np.ascontiguousarray(words), np.ascontiguousarray(byte.astype(np.uint8).reshape(k // 512, 16, n))


def unpack_weight(words, scales, fmt):
    g, p, n, _ = words.shape
    if fmt == "e4m3":
        vals = np.ascontiguousarray(words).view(ml_dtypes.float8_e4m3fn).astype(np.float64)
    else:
        nib = np.empty((g, p, n, 4), np.uint8)
        nib[..., 0::2] = words & 0xF
        nib[..., 1::2] = words >> 4
        vals = E2M1[nib]
    vals = vals * np.repeat(np.exp2(scales.astype(np.float64) - 127.0), 8, axis=1)[..., None]
    return vals.transpose(0, 1, 3, 2).reshape(g * 512, n)


B, IN, OUT, CHEBY_ORDER = 1024, 512, 512, 10


def silu(v):
    return v / (1.0 + np.exp(-v))


def chebyshev_bases(x, order):
    t0 = np.ones_like(x)
    if order == 1:
        return t0[None]
    ts = [t0, x]
    for _ in range(2, order):
        ts.append(2.0 * x * ts[-1] - ts[-2])
    return np.stack(ts)


def setup_inputs():
    u = np.minimum(mx_kscale(IN), 1.0) ** 2
    x = bf(np.random.random_sample((B, IN)) * u)
    base_weight = np.random.standard_normal((OUT, IN)) * 0.05 / u
    words, scales = pack_weight(np.ascontiguousarray(base_weight.T), "e4m3")
    cheby_weight = bf(np.random.standard_normal((OUT, IN, CHEBY_ORDER)) * 0.05)
    return {"x": x,
            "base_weight_words": words,
            "base_weight_scales": scales,
            "cheby_weight": cheby_weight}


def reference(x, base_weight_words, base_weight_scales, cheby_weight):
    x = f64(x)
    cheby_weight = f64(cheby_weight)
    b, n_in = x.shape
    n_out, _, o = cheby_weight.shape
    base_out = mxq(silu(x), 1, "e4m3") @ unpack_weight(base_weight_words, base_weight_scales, "e4m3")
    bases = chebyshev_bases(x, o)
    flat = bases.reshape(b, o * n_in)
    w = cheby_weight.reshape(n_out, n_in * o)
    spline_out = (mxq(flat, 1, "e4m3") @ mxq(w, 1, "e4m3").T) / o
    return base_out + spline_out

@@ -1,0 +1,301 @@
+from contextlib import ExitStack
+
+import concourse.mybir as mybir
+from concourse.masks import make_identity
+
+F32 = mybir.dt.float32
+BF16 = mybir.dt.bfloat16
+U32 = mybir.dt.uint32
+U8 = mybir.dt.uint8
+I32 = mybir.dt.int32
+FP8X4 = mybir.dt.float8_e4m3fn_x4
+ACT = mybir.ActivationFunctionType
+ALU = mybir.AluOpType
+
+P = 128
+B, IN, OUT, ORDERS = 1024, 512, 512, 10
+FLOPS = 2 * B * OUT * (IN * ORDERS + IN)
+Q = 104
+QUARTERS = ((0, 26), (26, 52), (52, 78), (78, 104))
+SPLITQ = {5: (26, 52, 78)}
+SCALAR_FINALS = (8,)
+MANUAL = True
+ORDER = (
+    ("ldx", 0), ("ldx", 1), ("xsp", 0), ("ldx", 2), ("xsp", 1), ("xev", 0),
+    ("ldx", 3), ("xsp", 2), ("xev", 1), ("ldw", 0), ("xsp", 3), ("xev", 2),
+    ("y", 0), ("xev", 3), ("F", 1, 0), ("y", 1), ("F", 1, 1), ("F", 1, 2),
+    ("ldw", 1), ("F", 1, 3), ("wt", 0, 0), ("y", 2), ("Qz", 0, 0, 8), ("wt", 0, 1),
+    ("y", 3), ("wt", 0, 2), ("Qz", 0, 8, 2), ("T3", 0), ("wt", 0, 3), ("ldw", 2),
+    ("wev", 0, 0), ("wt", 1, 0), ("T3", 1), ("wev", 0, 1), ("wt", 1, 1), ("wev", 0, 2),
+    ("wt", 1, 2), ("T3", 2), ("wev", 0, 3), ("wt", 1, 3), ("ldw", 3), ("wev", 1, 0),
+    ("wt", 2, 0), ("qw", 0), ("wev", 1, 1), ("wt", 2, 1), ("wev", 1, 2), ("wt", 2, 2),
+    ("T3", 3), ("wev", 1, 3), ("wt", 2, 3), ("ldw", 4), ("wev", 2, 0), ("wt", 3, 0),
+    ("qw", 1), ("wev", 2, 1), ("wt", 3, 1), ("wev", 2, 2), ("wt", 3, 2), ("wev", 2, 3),
+    ("F", 2, 0), ("wev", 3, 0), ("wt", 3, 3), ("ldW",), ("qw", 2), ("wev", 3, 1),
+    ("wt", 4, 0), ("wev", 3, 2), ("wt", 4, 1), ("F", 2, 1), ("wev", 3, 3), ("F", 2, 2),
+    ("wt", 4, 2), ("wev", 4, 0), ("wt", 4, 3), ("qw", 3), ("wev", 4, 1), ("xsi", 0),
+    ("wev", 4, 2), ("F", 2, 3), ("wev", 4, 3), ("xsi", 1), ("Qz", 1, 0, 8), ("s4", 0),
+    ("xsi", 2), ("qw", 4), ("s4", 1), ("xsi", 3), ("Qz", 1, 8, 2), ("s4", 2),
+    ("F", 3, 0), ("mm", 0, 0, 8), ("F", 3, 1), ("s4", 3), ("F", 3, 2), ("F", 3, 3),
+    ("silu", 0), ("Qz", 2, 0, 8), ("mm", 0, 8, 2), ("silu", 1), ("Qz", 2, 8, 2), ("mm", 1, 0, 8),
+    ("F", 4, 0), ("silu", 2), ("F", 4, 1), ("silu", 3), ("Qz", 3, 0, 8), ("mm", 1, 8, 2),
+    ("q5", 0), ("Qz", 3, 8, 2), ("qsilu",), ("q5", 1), ("F", 5, 0), ("mb", 0),
+    ("q5", 2), ("mb", 1), ("mm", 2, 0, 8), ("F", 5, 1), ("bev", 0), ("bev", 1),
+    ("epi", 0), ("q5", 3), ("epi", 1), ("st", 0), ("F", 5, 2), ("mm", 2, 8, 2),
+    ("st", 1), ("s6", 0), ("mb", 2), ("mm", 3, 0, 8), ("F", 5, 3), ("s6", 1),
+    ("F", 6, 0), ("F", 6, 1), ("s6", 2), ("Qz", 4, 0, 8), ("mm", 3, 8, 2), ("s6", 3),
+    ("Qz", 4, 8, 2), ("t7", 0), ("mb", 3), ("mm", 4, 0, 8), ("bev", 2), ("bev", 3),
+    ("F", 6, 2), ("s8", 0), ("F", 6, 3), ("epi", 2), ("mm", 4, 8, 2), ("epi", 3),
+    ("st", 2), ("mb", 4), ("t7", 1), ("st", 3), ("bev", 4), ("t7", 2),
+    ("s8", 1), ("t7", 3), ("s8", 2), ("F", 7, 0), ("s8", 3), ("F", 8, 2),
+    ("F", 8, 3), ("F", 7, 1), ("F", 7, 2), ("F", 7, 3), ("F", 8, 0), ("Qz", 5, 0, 8),
+    ("F", 8, 1), ("Qz", 5, 8, 2), ("mm", 5, 0, 8), ("epi", 4), ("F", 9, 0), ("st", 4),
+    ("mm", 5, 8, 2), ("mb", 5), ("Qz", 7, 0, 4), ("mb", 6), ("bev", 5), ("Qz", 7, 4, 2),
+    ("bev", 6), ("Qz", 6, 0, 8), ("mb", 7), ("mm", 7, 0, 4), ("Qz", 6, 8, 2), ("F", 9, 1),
+    ("mm", 7, 4, 2), ("mm", 6, 0, 8), ("Qz", 7, 6, 4), ("epi", 5), ("bev", 7), ("st", 5),
+    ("mm", 6, 8, 2), ("mm", 7, 6, 4), ("epi", 6), ("st", 6), ("epi", 7), ("st", 7),
+)
+
+
+def final_segments(n):
+    exact = n in (4, 9)
+    cuts = SPLITQ.get(n, ())
+    rows = []
+    for rho in range(10):
+        r0 = B * n + rho
+        c, m0 = r0 % 10, r0 // 10
+        cnt = (103 if rho < 4 else 102) if exact else Q
+        q = 0
+        while q < cnt:
+            mu, ml = divmod(m0 + q, P)
+            take = min([cnt - q, P - ml] + [k - q for k in cuts if k > q])
+            rows.append((mu, q, take, ml, rho, c))
+            q += take
+    segs = []
+    for mu, q, take, ml, rho, c in sorted(rows):
+        if segs:
+            last = segs[-1]
+            if last[:4] == [mu, q, take, ml] and last[4] + last[6] == rho and last[5] + last[6] == c:
+                last[6] += 1
+                continue
+        segs.append([mu, q, take, ml, rho, c, 1])
+    return segs
+
+
+def tile_kantlinear_kernel(tc, x, base_weight_words, base_weight_scales, cheby_weight, out):
+    nc = tc.nc
+    with ExitStack() as ctx:
+        keep = ctx.enter_context(tc.tile_pool(name="keep", bufs=1))
+        xrp = ctx.enter_context(tc.tile_pool(name="xrp", bufs=4))
+        wrp = ctx.enter_context(tc.tile_pool(name="wrp", bufs=3))
+        gwp = ctx.enter_context(tc.tile_pool(name="gwp", bufs=2))
+        gfp = ctx.enter_context(tc.tile_pool(name="gfp", bufs=3))
+        cfp = ctx.enter_context(tc.tile_pool(name="cfp", bufs=5))
+        epi = ctx.enter_context(tc.tile_pool(name="epi", bufs=2))
+        psp = ctx.enter_context(tc.psum_pool(name="psp", bufs=6))
+        bpp = ctx.enter_context(tc.psum_pool(name="bpp", bufs=2))
+        if MANUAL:
+            ctx.enter_context(tc.manual_schedule())
+
+        ident = keep.tile([P, P], F32, name="ident")
+        xs = keep.tile([P, 10, Q, 4], BF16, name="xs", align_bytes=64)
+        gs = keep.tile([P, B, 2, 2], BF16, name="gs", align_bytes=64)
+        cs = keep.tile([P, B], U32, name="cs", align_bytes=64)
+        ss = keep.tile([P, B], U8, name="ss", align_bytes=64)
+        ww = keep.tile([P, OUT], U32, name="ww", align_bytes=64)
+        ws = keep.tile([P, OUT], U8, name="ws", align_bytes=64)
+        cw = keep.tile([P, ORDERS, OUT], U32, name="cw", align_bytes=64)
+        sw = keep.tile([P, ORDERS, OUT], U8, name="sw", align_bytes=64)
+        ta = keep.tile([P, 10, Q, 4], F32, name="ta")
+        tb = keep.tile([P, 10, Q, 4], F32, name="tb")
+        t3 = keep.tile([P, 10, Q, 4], F32, name="t3")
+        td = keep.tile([P, 10, Q, 4], F32, name="td")
+        xsw = xs[:].bitcast(F32)
+        wv = cheby_weight.rearrange("o i k -> o (i k)")
+
+        make_identity(nc, ident[:])
+        nc.vector.memset(xsw[:, :, 102:104, :], 0.0)
+        nc.vector.memset(ws[:].bitcast(I32), 0)
+
+        live = {}
+
+        def get(kind, i, make):
+            if (kind, i) not in live:
+                live[(kind, i)] = make()
+            return live[(kind, i)]
+
+        def gf_tile(mu):
+            return get("gf", mu, lambda: gfp.tile([P, 10, P, 4], BF16, name="gf%d" % mu, tag="gf", align_bytes=64))
+
+        def cf_tile(mu):
+            return get("cf", mu, lambda: cfp.tile([P, 10 * P], U32, name="cf%d" % mu, tag="cf", align_bytes=64))
+
+        def sf_tile(mu):
+            return get("sf", mu, lambda: cfp.tile([P, 10 * P], U8, name="sf%d" % mu, tag="sf", align_bytes=64))
+
+        def ps_tile(kind, i):
+            return get(kind, i, lambda: psp.tile([P, 2, 256], F32, name="%s%d" % (kind, i), tag="ps"))
+
+        nc.vector.memset(gf_tile(0)[:], 1.0)
+
+        def ldx(k):
+            t = get("xr", k, lambda: xrp.tile([P, 2, IN], BF16, name="xr%d" % k, tag="xr"))
+            nc.sync.dma_start(out=t[:], in_=x[256 * k:256 * k + 256, :].rearrange("(a p) i -> p a i", p=P))
+
+        def ldw(g):
+            t = get("wr", g, lambda: wrp.tile([P, 4, 1024], BF16, name="wr%d" % g, tag="wr"))
+            nc.sync.dma_start(out=t[:], in_=wv[:, 1024 * g:1024 * g + 1024].rearrange("(h p) j -> p h j", p=P))
+
+        def ldbase():
+            nc.sync.dma_start(out=ww[:].bitcast(I32),
+                              in_=base_weight_words[0].rearrange("p n t -> p (n t)").bitcast(I32))
+            for qd in range(4):
+                nc.sync.dma_start(out=ws[32 * qd:32 * qd + 4, :].bitcast(I32),
+                                  in_=base_weight_scales[0, 4 * qd:4 * qd + 4, :].bitcast(I32))
+
+        def xsp(k):
+            tp = ps_tile("tpx", k)
+            for a in range(2):
+                xw = live[("xr", k)][:, a, :].bitcast(F32)
+                for u in range(2):
+                    nc.tensor.transpose(tp[:, u, P * a:P * a + P], xw[:, P * u:P * u + P], ident[:])
+
+        def xev(k):
+            tp = live[("tpx", k)]
+            b0 = 256 * k
+            q_lo = -(-b0 // 10)
+            q_hi = (b0 + 256) // 10
+            head = 10 * q_lo - b0
+            tail = b0 + 256 - 10 * q_hi
+            nc.vector.tensor_copy(out=xsw[:, :, q_lo:q_hi, :],
+                                  in_=tp[:, :, head:head + 10 * (q_hi - q_lo)].rearrange("p u (q r) -> p r q u", r=10))
+            if head:
+                nc.vector.tensor_copy(out=xsw[:, 10 - head:10, q_lo - 1, :],
+                                      in_=tp[:, :, 0:head].rearrange("p u r -> p r u"))
+            if tail:
+                nc.vector.tensor_copy(out=xsw[:, 0:tail, q_hi, :],
+                                      in_=tp[:, :, 256 - tail:256].rearrange("p u r -> p r u"))
+
+        def xsi(k):
+            tp = ps_tile("tps", k)
+            for a in range(2):
+                xw = live[("xr", k)][:, a, :].bitcast(F32)
+                for u in range(2):
+                    nc.tensor.transpose(tp[:, u, P * a:P * a + P], xw[:, u:256:2], ident[:])
+
+        def silu(k):
+            nc.scalar.activation(out=gs[:, 256 * k:256 * k + 256, :, :],
+                                 in_=live[("tps", k)][:].bitcast(BF16).rearrange("p u (b e) -> p b u e", e=2),
+                                 func=ACT.Silu)
+
+        def qsilu():
+            nc.vector.quantize_mx(out=cs[:].bitcast(FP8X4), scales=ss[:], in_=gs[:].rearrange("p b u e -> p (b u e)"))
+
+        def wt(g, h):
+            cc, hb = divmod(h, 2)
+            tp = ps_tile("tpw", 4 * g + h)
+            for a in range(2):
+                src = live[("wr", g)][:, 2 * hb + a, :].bitcast(F32)
+                for u in range(2):
+                    lo = 256 * cc + P * u
+                    nc.tensor.transpose(tp[:, u, P * a:P * a + P], src[:, lo:lo + P], ident[:])
+
+        def wev(g, h):
+            cc, hb = divmod(h, 2)
+            gw = get("gw", g, lambda: gwp.tile([P, 2, OUT, 4], BF16, name="gw%d" % g, tag="gw", align_bytes=64))
+            nc.scalar.copy(out=gw[:].bitcast(F32)[:, cc, 256 * hb:256 * hb + 256, :],
+                           in_=live[("tpw", 4 * g + h)][:].rearrange("p u o -> p o u"))
+
+        def qw(g):
+            nc.vector.quantize_mx(out=cw[:, 2 * g:2 * g + 2, :].rearrange("p c o -> p (c o)").bitcast(FP8X4),
+                                  scales=sw[:, 2 * g:2 * g + 2, :].rearrange("p c o -> p (c o)"),
+                                  in_=live[("gw", g)][:].rearrange("p c o t -> p (c o t)"))
+
+        def square(dst, src, scale, bias):
+            def run(j):
+                q0, q1 = QUARTERS[j]
+                nc.scalar.activation(out=dst[:, :, q0:q1, :], in_=src[:, :, q0:q1, :], func=ACT.Square,
+                                     bias=bias, scale=scale)
+            return run
+
+        def product(dst, in0, shift, in1):
+            def run(j):
+                q0, q1 = QUARTERS[j]
+                nc.vector.scalar_tensor_tensor(out=dst[:, :, q0:q1, :], in0=in0[:, :, q0:q1, :], scalar=shift,
+                                               in1=in1[:, :, q0:q1, :], op0=ALU.add, op1=ALU.mult)
+            return run
+
+        def affine(src):
+            def run(n, dst, sl):
+                if n in SCALAR_FINALS:
+                    nc.scalar.activation(out=dst, in_=sl(src), func=ACT.Copy, bias=-1.0, scale=0.5)
+                else:
+                    nc.vector.tensor_scalar(out=dst, in0=sl(src), scalar1=0.5, scalar2=-1.0, op0=ALU.mult, op1=ALU.add)
+            return run
+
+        def shifted_product(in0, shift, in1):
+            return lambda n, dst, sl: nc.vector.scalar_tensor_tensor(out=dst, in0=sl(in0), scalar=shift, in1=sl(in1),
+                                                                     op0=ALU.add, op1=ALU.mult)
+
+        emitters = {
+            1: lambda n, dst, sl: nc.vector.tensor_copy(out=dst, in_=sl(xs)),
+            2: affine(ta),
+            3: lambda n, dst, sl: nc.vector.tensor_copy(out=dst, in_=sl(t3)),
+            4: affine(tb),
+            5: shifted_product(ta, -1.25, xs),
+            6: affine(td),
+            7: lambda n, dst, sl: nc.vector.tensor_tensor(out=dst, in0=sl(ta), in1=sl(xs), op=ALU.subtract),
+            8: affine(tb),
+            9: shifted_product(td, -3.0, t3),
+        }
+
+        def final(n, i):
+            mu, q, take, ml, rho, c, nr = final_segments(n)[i]
+            emitters[n](n, gf_tile(mu)[:, c:c + nr, ml:ml + take, :], lambda t: t[:, rho:rho + nr, q:q + take, :])
+
+        def quantise_flat(mu, c0, ncs):
+            nc.vector.quantize_mx(
+                out=cf_tile(mu)[:, P * c0:P * (c0 + ncs)].bitcast(FP8X4),
+                scales=sf_tile(mu)[:, P * c0:P * (c0 + ncs)],
+                in_=gf_tile(mu)[:, c0:c0 + ncs, :, :].rearrange("p c m t -> p (c m t)"))
+
+        done = {}
+
+        def mm(mu, c0, ncs):
+            acc = ps_tile("acc", mu)
+            for c in range(c0, c0 + ncs):
+                done[mu] = done.get(mu, 0) + 1
+                nc.tensor.matmul_mx(out=acc[:].rearrange("p a b -> p (a b)"),
+                                    lhsT=cf_tile(mu)[:, P * c:P * c + P].bitcast(FP8X4),
+                                    lhsT_scale=sf_tile(mu)[:, P * c:P * c + P],
+                                    rhs=cw[:, c, :].bitcast(FP8X4), rhs_scale=sw[:, c, :],
+                                    start=(done[mu] == 1), stop=(done[mu] == ORDERS))
+
+        def mb(mu):
+            bp = get("bp", mu, lambda: bpp.tile([P, OUT], F32, name="bp%d" % mu, tag="bp"))
+            nc.tensor.matmul_mx(out=bp[:], lhsT=cs[:, P * mu:P * mu + P].bitcast(FP8X4),
+                                lhsT_scale=ss[:, P * mu:P * mu + P],
+                                rhs=ww[:].bitcast(FP8X4), rhs_scale=ws[:], start=True, stop=True)
+
+        def bev(mu):
+            bs = get("bs", mu, lambda: epi.tile([P, OUT], F32, name="bs%d" % mu, tag="bs"))
+            nc.scalar.copy(out=bs[:], in_=live[("bp", mu)][:])
+
+        def epilogue(mu):
+            ot = get("ot", mu, lambda: epi.tile([P, OUT], F32, name="ot%d" % mu, tag="ot"))
+            nc.vector.scalar_tensor_tensor(out=ot[:], in0=live[("acc", mu)][:].rearrange("p a b -> p (a b)"), scalar=0.1,
+                                           in1=live[("bs", mu)][:], op0=ALU.mult, op1=ALU.add)
+
+        def store(mu):
+            nc.sync.dma_start(out=out[P * mu:P * mu + P, :], in_=live[("ot", mu)][:])
+
+        steps = {
+            "ldx": ldx, "ldw": ldw, "ldW": ldbase, "xsp": xsp, "xev": xev, "xsi": xsi, "silu": silu, "qsilu": qsilu,
+            "wt": wt, "wev": wev, "qw": qw,
+            "y": square(ta, xs, 2.0, 0.0), "s4": square(tb, ta, 1.0, -2.0), "q5": square(ta, ta, 1.0, -2.5),
+            "s6": square(td, t3, 2.0, 0.0), "s8": square(tb, tb, 1.0, -2.0),
+            "T3": product(t3, ta, -3.0, xs), "t7": product(ta, tb, -2.0, t3),
+            "F": final, "Qz": quantise_flat, "mm": mm, "mb": mb, "bev": bev, "epi": epilogue, "st": store,
+        }
+        for name in ORDER:
+            steps[name[0]](*name[1:])

@@ -17,43 +17,41 @@ B, IN, OUT, ORDERS = 1024, 512, 512, 10
 FLOPS = 2 * B * OUT * (IN * ORDERS + IN)
 Q = 104
 QUARTERS = ((0, 26), (26, 52), (52, 78), (78, 104))
-SPLITQ = {5: (26, 52, 78)}
+SPLITQ = {5: (52,)}
 SCALAR_FINALS = (8,)
 MANUAL = True
 ORDER = (
     ("ldx", 0), ("ldx", 1), ("xsp", 0), ("ldx", 2), ("xsp", 1), ("xev", 0),
     ("ldx", 3), ("xsp", 2), ("xev", 1), ("ldw", 0), ("xsp", 3), ("xev", 2),
-    ("y", 0), ("xev", 3), ("F", 1, 0), ("y", 1), ("F", 1, 1), ("F", 1, 2),
-    ("ldw", 1), ("F", 1, 3), ("wt", 0, 0), ("y", 2), ("Qz", 0, 0, 8), ("wt", 0, 1),
-    ("y", 3), ("wt", 0, 2), ("Qz", 0, 8, 2), ("T3", 0), ("wt", 0, 3), ("ldw", 2),
-    ("wev", 0, 0), ("wt", 1, 0), ("T3", 1), ("wev", 0, 1), ("wt", 1, 1), ("wev", 0, 2),
-    ("wt", 1, 2), ("T3", 2), ("wev", 0, 3), ("wt", 1, 3), ("ldw", 3), ("wev", 1, 0),
-    ("wt", 2, 0), ("qw", 0), ("wev", 1, 1), ("wt", 2, 1), ("wev", 1, 2), ("wt", 2, 2),
-    ("T3", 3), ("wev", 1, 3), ("wt", 2, 3), ("ldw", 4), ("wev", 2, 0), ("wt", 3, 0),
-    ("qw", 1), ("wev", 2, 1), ("wt", 3, 1), ("wev", 2, 2), ("wt", 3, 2), ("wev", 2, 3),
-    ("F", 2, 0), ("wev", 3, 0), ("wt", 3, 3), ("ldW",), ("qw", 2), ("wev", 3, 1),
-    ("wt", 4, 0), ("wev", 3, 2), ("wt", 4, 1), ("F", 2, 1), ("wev", 3, 3), ("F", 2, 2),
-    ("wt", 4, 2), ("wev", 4, 0), ("wt", 4, 3), ("qw", 3), ("wev", 4, 1), ("xsi", 0),
-    ("wev", 4, 2), ("F", 2, 3), ("wev", 4, 3), ("xsi", 1), ("Qz", 1, 0, 8), ("s4", 0),
-    ("xsi", 2), ("qw", 4), ("s4", 1), ("xsi", 3), ("Qz", 1, 8, 2), ("s4", 2),
-    ("F", 3, 0), ("mm", 0, 0, 8), ("F", 3, 1), ("s4", 3), ("F", 3, 2), ("F", 3, 3),
-    ("silu", 0), ("Qz", 2, 0, 8), ("mm", 0, 8, 2), ("silu", 1), ("Qz", 2, 8, 2), ("mm", 1, 0, 8),
-    ("F", 4, 0), ("silu", 2), ("F", 4, 1), ("silu", 3), ("Qz", 3, 0, 8), ("mm", 1, 8, 2),
-    ("q5", 0), ("Qz", 3, 8, 2), ("qsilu",), ("q5", 1), ("F", 5, 0), ("mb", 0),
-    ("q5", 2), ("mb", 1), ("mm", 2, 0, 8), ("F", 5, 1), ("bev", 0), ("bev", 1),
-    ("epi", 0), ("q5", 3), ("epi", 1), ("st", 0), ("F", 5, 2), ("mm", 2, 8, 2),
-    ("st", 1), ("s6", 0), ("mb", 2), ("mm", 3, 0, 8), ("F", 5, 3), ("s6", 1),
-    ("F", 6, 0), ("F", 6, 1), ("s6", 2), ("Qz", 4, 0, 8), ("mm", 3, 8, 2), ("s6", 3),
-    ("Qz", 4, 8, 2), ("t7", 0), ("mb", 3), ("mm", 4, 0, 8), ("bev", 2), ("bev", 3),
-    ("F", 6, 2), ("s8", 0), ("F", 6, 3), ("epi", 2), ("mm", 4, 8, 2), ("epi", 3),
-    ("st", 2), ("mb", 4), ("t7", 1), ("st", 3), ("bev", 4), ("t7", 2),
-    ("s8", 1), ("t7", 3), ("s8", 2), ("F", 7, 0), ("s8", 3), ("F", 8, 2),
-    ("F", 8, 3), ("F", 7, 1), ("F", 7, 2), ("F", 7, 3), ("F", 8, 0), ("Qz", 5, 0, 8),
-    ("F", 8, 1), ("Qz", 5, 8, 2), ("mm", 5, 0, 8), ("epi", 4), ("F", 9, 0), ("st", 4),
-    ("mm", 5, 8, 2), ("mb", 5), ("Qz", 7, 0, 4), ("mb", 6), ("bev", 5), ("Qz", 7, 4, 2),
-    ("bev", 6), ("Qz", 6, 0, 8), ("mb", 7), ("mm", 7, 0, 4), ("Qz", 6, 8, 2), ("F", 9, 1),
-    ("mm", 7, 4, 2), ("mm", 6, 0, 8), ("Qz", 7, 6, 4), ("epi", 5), ("bev", 7), ("st", 5),
-    ("mm", 6, 8, 2), ("mm", 7, 6, 4), ("epi", 6), ("st", 6), ("epi", 7), ("st", 7),
+    ("y", 0, 1), ("xev", 3), ("y", 1, 2), ("F", 1, 0), ("F", 1, 1), ("ldw", 1),
+    ("F", 1, 2), ("F", 1, 3), ("wt", 0, 0), ("y", 2, 3), ("Qz", 0, 0, 8), ("wt", 0, 1),
+    ("wt", 0, 2), ("y", 3, 4), ("wt", 0, 3), ("Qz", 0, 8, 2), ("T3", 0, 2), ("ldw", 2),
+    ("wev", 0, 0), ("wt", 1, 0), ("wev", 0, 1), ("wt", 1, 1), ("wev", 0, 2), ("wt", 1, 2),
+    ("wev", 0, 3), ("T3", 2, 4), ("wt", 1, 3), ("ldw", 3), ("wev", 1, 0), ("wt", 2, 0),
+    ("wev", 1, 1), ("wt", 2, 1), ("wev", 1, 2), ("wt", 2, 2), ("F", 2, 0), ("wev", 1, 3),
+    ("wt", 2, 3), ("s4", 0, 2), ("ldw", 4), ("F", 2, 1), ("F", 2, 2), ("wt", 3, 0),
+    ("wt", 3, 1), ("F", 2, 3), ("qw", 0), ("ldW",), ("qw", 1), ("wev", 2, 0),
+    ("wev", 2, 1), ("wt", 3, 2), ("Qz", 1, 0, 8), ("wev", 2, 2), ("wt", 3, 3), ("wev", 2, 3),
+    ("wt", 4, 0), ("Qz", 1, 8, 2), ("s4", 2, 4), ("wt", 4, 1), ("F", 3, 0), ("F", 3, 1),
+    ("F", 3, 2), ("F", 3, 3), ("wev", 3, 0), ("qw", 2), ("wev", 3, 1), ("wt", 4, 2),
+    ("wev", 3, 2), ("wt", 4, 3), ("Qz", 2, 0, 8), ("wev", 3, 3), ("xsi", 0), ("wev", 4, 0),
+    ("Qz", 2, 8, 2), ("xsi", 1), ("wev", 4, 1), ("F", 4, 0), ("wev", 4, 2), ("xsi", 2),
+    ("wev", 4, 3), ("F", 4, 1), ("q5", 0, 2), ("xsi", 3), ("qw", 3), ("qw", 4),
+    ("mm", 0, 0, 8), ("q5", 2, 4), ("Qz", 3, 0, 8), ("Qz", 3, 8, 2), ("s6", 0, 2), ("mm", 0, 8, 2),
+    ("F", 5, 0), ("mm", 1, 0, 8), ("s6", 2, 4), ("F", 5, 1), ("mm", 1, 8, 2), ("silu", 0),
+    ("t7", 0, 2), ("silu", 1), ("mm", 2, 0, 8), ("silu", 2), ("t7", 2, 4), ("silu", 3),
+    ("mm", 2, 8, 2), ("mm", 3, 0, 8), ("s8", 0, 2), ("F", 6, 0), ("F", 6, 1), ("F", 6, 2),
+    ("F", 6, 3), ("s8", 2, 4), ("Qz", 4, 0, 8), ("mm", 3, 8, 2), ("Qz", 4, 8, 2), ("mm", 4, 0, 8),
+    ("F", 7, 0), ("F", 8, 2), ("F", 8, 3), ("F", 7, 1), ("qsilu",), ("mm", 4, 8, 2),
+    ("F", 7, 2), ("mb", 0), ("mb", 1), ("bev", 0), ("bev", 1), ("mb", 2),
+    ("F", 7, 3), ("mb", 3), ("F", 8, 0), ("Qz", 5, 0, 8), ("F", 8, 1), ("Qz", 5, 8, 2),
+    ("mm", 5, 0, 8), ("F", 9, 0), ("bev", 2), ("bev", 3), ("mm", 5, 8, 2), ("Qz", 6, 0, 8),
+    ("mb", 4), ("mb", 5), ("bev", 4), ("Qz", 6, 8, 2), ("bev", 5), ("epi", 0),
+    ("epi", 1), ("st", 0), ("mm", 6, 0, 8), ("Qz", 7, 0, 4), ("st", 1), ("Qz", 7, 4, 2),
+    ("F", 9, 1), ("mm", 6, 8, 2), ("mm", 7, 0, 4), ("epi", 2), ("epi", 3), ("st", 2),
+    ("Qz", 7, 6, 4), ("mm", 7, 4, 2), ("st", 3), ("epi", 4), ("mb", 6), ("mb", 7),
+    ("bev", 6), ("epi", 5), ("mm", 7, 6, 4), ("st", 4), ("bev", 7), ("epi", 6),
+    ("st", 5), ("st", 6), ("epi", 7), ("st", 7),
 )
 
 
@@ -91,7 +89,7 @@ def tile_kantlinear_kernel(tc, x, base_weight_words, base_weight_scales, cheby_w
         gwp = ctx.enter_context(tc.tile_pool(name="gwp", bufs=2))
         gfp = ctx.enter_context(tc.tile_pool(name="gfp", bufs=3))
         cfp = ctx.enter_context(tc.tile_pool(name="cfp", bufs=5))
-        epi = ctx.enter_context(tc.tile_pool(name="epi", bufs=2))
+        epi = ctx.enter_context(tc.tile_pool(name="epi", bufs=6))
         psp = ctx.enter_context(tc.psum_pool(name="psp", bufs=6))
         bpp = ctx.enter_context(tc.psum_pool(name="bpp", bufs=2))
         if MANUAL:
@@ -212,15 +210,15 @@ def tile_kantlinear_kernel(tc, x, base_weight_words, base_weight_scales, cheby_w
                                   in_=live[("gw", g)][:].rearrange("p c o t -> p (c o t)"))
 
         def square(dst, src, scale, bias):
-            def run(j):
-                q0, q1 = QUARTERS[j]
+            def run(j0, j1):
+                q0, q1 = QUARTERS[j0][0], QUARTERS[j1 - 1][1]
                 nc.scalar.activation(out=dst[:, :, q0:q1, :], in_=src[:, :, q0:q1, :], func=ACT.Square,
                                      bias=bias, scale=scale)
             return run
 
         def product(dst, in0, shift, in1):
-            def run(j):
-                q0, q1 = QUARTERS[j]
+            def run(j0, j1):
+                q0, q1 = QUARTERS[j0][0], QUARTERS[j1 - 1][1]
                 nc.vector.scalar_tensor_tensor(out=dst[:, :, q0:q1, :], in0=in0[:, :, q0:q1, :], scalar=shift,
                                                in1=in1[:, :, q0:q1, :], op0=ALU.add, op1=ALU.mult)
             return run
@@ -282,12 +280,11 @@ def tile_kantlinear_kernel(tc, x, base_weight_words, base_weight_scales, cheby_w
             nc.scalar.copy(out=bs[:], in_=live[("bp", mu)][:])
 
         def epilogue(mu):
-            ot = get("ot", mu, lambda: epi.tile([P, OUT], F32, name="ot%d" % mu, tag="ot"))
-            nc.vector.scalar_tensor_tensor(out=ot[:], in0=live[("acc", mu)][:].rearrange("p a b -> p (a b)"), scalar=0.1,
+            nc.vector.scalar_tensor_tensor(out=live[("bs", mu)][:], in0=live[("acc", mu)][:].rearrange("p a b -> p (a b)"), scalar=0.1,
                                            in1=live[("bs", mu)][:], op0=ALU.mult, op1=ALU.add)
 
         def store(mu):
-            nc.sync.dma_start(out=out[P * mu:P * mu + P, :], in_=live[("ot", mu)][:])
+            nc.sync.dma_start(out=out[P * mu:P * mu + P, :], in_=live[("bs", mu)][:])
 
         steps = {
             "ldx": ldx, "ldw": ldw, "ldW": ldbase, "xsp": xsp, "xev": xev, "xsi": xsi, "silu": silu, "qsilu": qsilu,

@@ -18,7 +18,7 @@ FLOPS = 2 * B * OUT * (IN * ORDERS + IN)
 Q = 104
 QUARTERS = ((0, 26), (26, 52), (52, 78), (78, 104))
 SPLITQ = {5: (52,)}
-SCALAR_FINALS = (8,)
+SCALAR_FINALS = (6, 8)
 MANUAL = True
 ORDER = (
     ("ldx", 0), ("ldx", 1), ("xsp", 0), ("ldx", 2), ("xsp", 1), ("xev", 0),
@@ -29,29 +29,29 @@ ORDER = (
     ("wev", 0, 0), ("wt", 1, 0), ("wev", 0, 1), ("wt", 1, 1), ("wev", 0, 2), ("wt", 1, 2),
     ("wev", 0, 3), ("T3", 2, 4), ("wt", 1, 3), ("ldw", 3), ("wev", 1, 0), ("wt", 2, 0),
     ("wev", 1, 1), ("wt", 2, 1), ("wev", 1, 2), ("wt", 2, 2), ("F", 2, 0), ("wev", 1, 3),
-    ("wt", 2, 3), ("s4", 0, 2), ("ldw", 4), ("F", 2, 1), ("F", 2, 2), ("wt", 3, 0),
-    ("wt", 3, 1), ("F", 2, 3), ("qw", 0), ("ldW",), ("qw", 1), ("wev", 2, 0),
-    ("wev", 2, 1), ("wt", 3, 2), ("Qz", 1, 0, 8), ("wev", 2, 2), ("wt", 3, 3), ("wev", 2, 3),
-    ("wt", 4, 0), ("Qz", 1, 8, 2), ("s4", 2, 4), ("wt", 4, 1), ("F", 3, 0), ("F", 3, 1),
-    ("F", 3, 2), ("F", 3, 3), ("wev", 3, 0), ("qw", 2), ("wev", 3, 1), ("wt", 4, 2),
-    ("wev", 3, 2), ("wt", 4, 3), ("Qz", 2, 0, 8), ("wev", 3, 3), ("xsi", 0), ("wev", 4, 0),
-    ("Qz", 2, 8, 2), ("xsi", 1), ("wev", 4, 1), ("F", 4, 0), ("wev", 4, 2), ("xsi", 2),
-    ("wev", 4, 3), ("F", 4, 1), ("q5", 0, 2), ("xsi", 3), ("qw", 3), ("qw", 4),
-    ("mm", 0, 0, 8), ("q5", 2, 4), ("Qz", 3, 0, 8), ("Qz", 3, 8, 2), ("s6", 0, 2), ("mm", 0, 8, 2),
-    ("F", 5, 0), ("mm", 1, 0, 8), ("s6", 2, 4), ("F", 5, 1), ("mm", 1, 8, 2), ("silu", 0),
-    ("t7", 0, 2), ("silu", 1), ("mm", 2, 0, 8), ("silu", 2), ("t7", 2, 4), ("silu", 3),
-    ("mm", 2, 8, 2), ("mm", 3, 0, 8), ("s8", 0, 2), ("F", 6, 0), ("F", 6, 1), ("F", 6, 2),
-    ("F", 6, 3), ("s8", 2, 4), ("Qz", 4, 0, 8), ("mm", 3, 8, 2), ("Qz", 4, 8, 2), ("mm", 4, 0, 8),
-    ("F", 7, 0), ("F", 8, 2), ("F", 8, 3), ("F", 7, 1), ("qsilu",), ("mm", 4, 8, 2),
-    ("F", 7, 2), ("mb", 0), ("mb", 1), ("bev", 0), ("bev", 1), ("mb", 2),
-    ("F", 7, 3), ("mb", 3), ("F", 8, 0), ("Qz", 5, 0, 8), ("F", 8, 1), ("Qz", 5, 8, 2),
-    ("mm", 5, 0, 8), ("F", 9, 0), ("bev", 2), ("bev", 3), ("mm", 5, 8, 2), ("Qz", 6, 0, 8),
-    ("mb", 4), ("mb", 5), ("bev", 4), ("Qz", 6, 8, 2), ("bev", 5), ("epi", 0),
-    ("epi", 1), ("st", 0), ("mm", 6, 0, 8), ("Qz", 7, 0, 4), ("st", 1), ("Qz", 7, 4, 2),
-    ("F", 9, 1), ("mm", 6, 8, 2), ("mm", 7, 0, 4), ("epi", 2), ("epi", 3), ("st", 2),
-    ("Qz", 7, 6, 4), ("mm", 7, 4, 2), ("st", 3), ("epi", 4), ("mb", 6), ("mb", 7),
-    ("bev", 6), ("epi", 5), ("mm", 7, 6, 4), ("st", 4), ("bev", 7), ("epi", 6),
-    ("st", 5), ("st", 6), ("epi", 7), ("st", 7),
+    ("wt", 2, 3), ("s4", 0, 2), ("ldw", 4), ("F", 2, 1), ("qw", 0), ("wt", 3, 0),
+    ("wt", 3, 1), ("qw", 1), ("wev", 2, 0), ("ldW",), ("wev", 2, 1), ("Qz", 1, 0, 8),
+    ("wt", 3, 2), ("wev", 2, 2), ("wt", 3, 3), ("wev", 2, 3), ("Qz", 1, 8, 2), ("wt", 4, 0),
+    ("F", 2, 2), ("s4", 2, 4), ("wt", 4, 1), ("F", 2, 3), ("F", 3, 0), ("F", 3, 1),
+    ("wev", 3, 0), ("F", 3, 2), ("wev", 3, 1), ("wt", 4, 2), ("F", 3, 3), ("wev", 3, 2),
+    ("qw", 2), ("wt", 4, 3), ("wev", 3, 3), ("xsi", 0), ("q5", 0, 2), ("Qz", 2, 0, 8),
+    ("xsi", 1), ("Qz", 2, 8, 2), ("F", 4, 0), ("wev", 4, 0), ("wev", 4, 1), ("xsi", 2),
+    ("F", 4, 1), ("wev", 4, 2), ("qw", 3), ("xsi", 3), ("wev", 4, 3), ("q5", 2, 4),
+    ("qw", 4), ("mm", 0, 0, 8), ("Qz", 3, 0, 8), ("s6", 0, 2), ("Qz", 3, 8, 2), ("mm", 0, 8, 2),
+    ("F", 5, 0), ("mm", 1, 0, 8), ("s6", 2, 4), ("F", 5, 1), ("mm", 1, 8, 2), ("F", 6, 2),
+    ("t7", 0, 2), ("F", 6, 3), ("t7", 2, 4), ("F", 6, 0), ("F", 6, 1), ("silu", 0),
+    ("Qz", 4, 0, 8), ("silu", 1), ("mm", 2, 0, 8), ("Qz", 4, 8, 2), ("silu", 2), ("F", 7, 0),
+    ("silu", 3), ("mm", 2, 8, 2), ("F", 7, 1), ("mm", 3, 0, 8), ("s8", 0, 2), ("F", 7, 2),
+    ("F", 7, 3), ("s8", 2, 4), ("qsilu",), ("mm", 3, 8, 2), ("mm", 4, 0, 8), ("Qz", 5, 0, 8),
+    ("F", 8, 2), ("F", 8, 3), ("Qz", 5, 8, 2), ("F", 8, 0), ("mm", 4, 8, 2), ("F", 9, 0),
+    ("mb", 0), ("F", 8, 1), ("mb", 1), ("mm", 5, 0, 8), ("bev", 0), ("Qz", 6, 0, 8),
+    ("mm", 5, 8, 2), ("bev", 1), ("mb", 2), ("Qz", 6, 8, 2), ("mb", 3), ("epi", 0),
+    ("bev", 2), ("epi", 1), ("bev", 3), ("st", 0), ("mm", 6, 0, 8), ("Qz", 7, 0, 4),
+    ("st", 1), ("Qz", 7, 4, 2), ("F", 9, 1), ("mm", 6, 8, 2), ("mb", 4), ("Qz", 7, 6, 4),
+    ("mb", 5), ("bev", 4), ("mm", 7, 0, 4), ("epi", 2), ("bev", 5), ("epi", 3),
+    ("st", 2), ("mm", 7, 4, 2), ("epi", 4), ("st", 3), ("mb", 6), ("epi", 5),
+    ("st", 4), ("mb", 7), ("bev", 6), ("mm", 7, 6, 4), ("st", 5), ("bev", 7),
+    ("epi", 6), ("st", 6), ("epi", 7), ("st", 7),
 )
 
 

@@ -18,40 +18,40 @@ FLOPS = 2 * B * OUT * (IN * ORDERS + IN)
 Q = 104
 QUARTERS = ((0, 26), (26, 52), (52, 78), (78, 104))
 SPLITQ = {5: (52,)}
-SCALAR_FINALS = (6, 8)
+SCALAR_FINALS = ((6, 4), (8, 6), (8, 7))
 MANUAL = True
 ORDER = (
     ("ldx", 0), ("ldx", 1), ("xsp", 0), ("ldx", 2), ("xsp", 1), ("xev", 0),
     ("ldx", 3), ("xsp", 2), ("xev", 1), ("ldw", 0), ("xsp", 3), ("xev", 2),
-    ("y", 0, 1), ("xev", 3), ("y", 1, 2), ("F", 1, 0), ("F", 1, 1), ("ldw", 1),
-    ("F", 1, 2), ("F", 1, 3), ("wt", 0, 0), ("y", 2, 3), ("Qz", 0, 0, 8), ("wt", 0, 1),
-    ("wt", 0, 2), ("y", 3, 4), ("wt", 0, 3), ("Qz", 0, 8, 2), ("T3", 0, 2), ("ldw", 2),
-    ("wev", 0, 0), ("wt", 1, 0), ("wev", 0, 1), ("wt", 1, 1), ("wev", 0, 2), ("wt", 1, 2),
-    ("wev", 0, 3), ("T3", 2, 4), ("wt", 1, 3), ("ldw", 3), ("wev", 1, 0), ("wt", 2, 0),
-    ("wev", 1, 1), ("wt", 2, 1), ("wev", 1, 2), ("wt", 2, 2), ("F", 2, 0), ("wev", 1, 3),
-    ("wt", 2, 3), ("s4", 0, 2), ("ldw", 4), ("F", 2, 1), ("qw", 0), ("wt", 3, 0),
-    ("wt", 3, 1), ("qw", 1), ("wev", 2, 0), ("ldW",), ("wev", 2, 1), ("Qz", 1, 0, 8),
-    ("wt", 3, 2), ("wev", 2, 2), ("wt", 3, 3), ("wev", 2, 3), ("Qz", 1, 8, 2), ("wt", 4, 0),
-    ("F", 2, 2), ("s4", 2, 4), ("wt", 4, 1), ("F", 2, 3), ("F", 3, 0), ("F", 3, 1),
-    ("wev", 3, 0), ("F", 3, 2), ("wev", 3, 1), ("wt", 4, 2), ("F", 3, 3), ("wev", 3, 2),
-    ("qw", 2), ("wt", 4, 3), ("wev", 3, 3), ("xsi", 0), ("q5", 0, 2), ("Qz", 2, 0, 8),
-    ("xsi", 1), ("Qz", 2, 8, 2), ("F", 4, 0), ("wev", 4, 0), ("wev", 4, 1), ("xsi", 2),
-    ("F", 4, 1), ("wev", 4, 2), ("qw", 3), ("xsi", 3), ("wev", 4, 3), ("q5", 2, 4),
-    ("qw", 4), ("mm", 0, 0, 8), ("Qz", 3, 0, 8), ("s6", 0, 2), ("Qz", 3, 8, 2), ("mm", 0, 8, 2),
-    ("F", 5, 0), ("mm", 1, 0, 8), ("s6", 2, 4), ("F", 5, 1), ("mm", 1, 8, 2), ("F", 6, 2),
-    ("t7", 0, 2), ("F", 6, 3), ("t7", 2, 4), ("F", 6, 0), ("F", 6, 1), ("silu", 0),
-    ("Qz", 4, 0, 8), ("silu", 1), ("mm", 2, 0, 8), ("Qz", 4, 8, 2), ("silu", 2), ("F", 7, 0),
-    ("silu", 3), ("mm", 2, 8, 2), ("F", 7, 1), ("mm", 3, 0, 8), ("s8", 0, 2), ("F", 7, 2),
-    ("F", 7, 3), ("s8", 2, 4), ("qsilu",), ("mm", 3, 8, 2), ("mm", 4, 0, 8), ("Qz", 5, 0, 8),
-    ("F", 8, 2), ("F", 8, 3), ("Qz", 5, 8, 2), ("F", 8, 0), ("mm", 4, 8, 2), ("F", 9, 0),
-    ("mb", 0), ("F", 8, 1), ("mb", 1), ("mm", 5, 0, 8), ("bev", 0), ("Qz", 6, 0, 8),
-    ("mm", 5, 8, 2), ("bev", 1), ("mb", 2), ("Qz", 6, 8, 2), ("mb", 3), ("epi", 0),
-    ("bev", 2), ("epi", 1), ("bev", 3), ("st", 0), ("mm", 6, 0, 8), ("Qz", 7, 0, 4),
-    ("st", 1), ("Qz", 7, 4, 2), ("F", 9, 1), ("mm", 6, 8, 2), ("mb", 4), ("Qz", 7, 6, 4),
-    ("mb", 5), ("bev", 4), ("mm", 7, 0, 4), ("epi", 2), ("bev", 5), ("epi", 3),
-    ("st", 2), ("mm", 7, 4, 2), ("epi", 4), ("st", 3), ("mb", 6), ("epi", 5),
-    ("st", 4), ("mb", 7), ("bev", 6), ("mm", 7, 6, 4), ("st", 5), ("bev", 7),
-    ("epi", 6), ("st", 6), ("epi", 7), ("st", 7),
+    ("y", 0, 1), ("F", 1, 0), ("F", 1, 1), ("xev", 3), ("y", 1, 2), ("Qz", 0, 0, 8),
+    ("ldw", 1), ("wt", 0, 0), ("y", 2, 3), ("Qz", 0, 8, 2), ("T3", 0, 2), ("wt", 0, 1),
+    ("y", 3, 4), ("wt", 0, 2), ("wt", 0, 3), ("ldw", 2), ("wev", 0, 0), ("wt", 1, 0),
+    ("F", 1, 2), ("wev", 0, 1), ("F", 1, 3), ("wt", 1, 1), ("wev", 0, 2), ("T3", 2, 4),
+    ("wt", 1, 2), ("wev", 0, 3), ("wt", 1, 3), ("ldw", 3), ("wev", 1, 0), ("wt", 2, 0),
+    ("wev", 1, 1), ("wt", 2, 1), ("qw", 0), ("wev", 1, 2), ("wt", 2, 2), ("wev", 1, 3),
+    ("F", 2, 0), ("wt", 2, 3), ("ldw", 4), ("wev", 2, 0), ("wt", 3, 0), ("F", 2, 1),
+    ("wev", 2, 1), ("qw", 1), ("wt", 3, 1), ("wev", 2, 2), ("wt", 3, 2), ("Qz", 1, 0, 8),
+    ("wev", 2, 3), ("wt", 3, 3), ("ldW",), ("s4", 2, 4), ("wt", 4, 0), ("Qz", 1, 8, 2),
+    ("qw", 2), ("wt", 4, 1), ("F", 2, 2), ("wev", 3, 0), ("F", 2, 3), ("wev", 3, 1),
+    ("wt", 4, 2), ("F", 3, 2), ("F", 3, 3), ("wev", 3, 2), ("wt", 4, 3), ("F", 3, 0),
+    ("F", 3, 1), ("wev", 3, 3), ("xsi", 0), ("s4", 0, 2), ("qw", 3), ("xsi", 1),
+    ("Qz", 2, 0, 8), ("wev", 4, 0), ("Qz", 2, 8, 2), ("wev", 4, 1), ("xsi", 2), ("F", 4, 0),
+    ("wev", 4, 2), ("xsi", 3), ("wev", 4, 3), ("F", 4, 1), ("q5", 0, 2), ("mm", 1, 0, 8),
+    ("qw", 4), ("Qz", 3, 0, 8), ("q5", 2, 4), ("Qz", 3, 8, 2), ("F", 5, 0), ("mm", 1, 8, 2),
+    ("mm", 0, 0, 8), ("s6", 2, 4), ("F", 5, 1), ("mm", 0, 8, 2), ("s6", 0, 2), ("t7", 0, 2),
+    ("silu", 0), ("F", 6, 2), ("silu", 1), ("mm", 3, 0, 8), ("F", 6, 3), ("silu", 2),
+    ("t7", 2, 4), ("silu", 3), ("F", 7, 0), ("mm", 3, 8, 2), ("F", 6, 0), ("mm", 2, 0, 8),
+    ("F", 6, 1), ("s8", 0, 2), ("F", 7, 1), ("qsilu",), ("mm", 2, 8, 2), ("Qz", 4, 0, 8),
+    ("mb", 0), ("s8", 2, 4), ("mb", 1), ("Qz", 4, 8, 2), ("mm", 4, 0, 8), ("Qz", 5, 0, 8),
+    ("F", 8, 2), ("Qz", 5, 8, 2), ("F", 8, 3), ("F", 7, 2), ("mm", 4, 8, 2), ("bev", 0),
+    ("bev", 1), ("mb", 2), ("F", 7, 3), ("F", 9, 0), ("F", 8, 0), ("mb", 3),
+    ("mm", 5, 0, 8), ("F", 8, 1), ("epi", 0), ("mm", 5, 8, 2), ("epi", 1), ("st", 0),
+    ("bev", 2), ("Qz", 6, 0, 8), ("st", 1), ("bev", 3), ("mb", 4), ("bev", 4),
+    ("mb", 5), ("Qz", 6, 8, 2), ("mm", 6, 0, 8), ("Qz", 7, 0, 4), ("bev", 5), ("Qz", 7, 4, 2),
+    ("F", 9, 1), ("mm", 6, 8, 2), ("mm", 7, 0, 4), ("epi", 2), ("epi", 3), ("st", 2),
+    ("mm", 7, 4, 2), ("Qz", 7, 6, 4), ("st", 3), ("mb", 6), ("epi", 4), ("mb", 7),
+    ("bev", 6), ("mm", 7, 6, 4), ("epi", 5), ("st", 4), ("bev", 7), ("epi", 6),
+    ("st", 5), ("epi", 7), ("st", 6), ("st", 7),
 )
 
 
@@ -249,7 +249,7 @@ def tile_kantlinear_kernel(tc, x, base_weight_words, base_weight_scales, cheby_w
 
         def final(n, i):
             mu, q, take, ml, rho, c, nr = final_segments(n)[i]
-            emitters[n](n, gf_tile(mu)[:, c:c + nr, ml:ml + take, :], lambda t: t[:, rho:rho + nr, q:q + take, :])
+            emitters[n]((n, mu), gf_tile(mu)[:, c:c + nr, ml:ml + take, :], lambda t: t[:, rho:rho + nr, q:q + take, :])
 
         def quantise_flat(mu, c0, ncs):
             nc.vector.quantize_mx(

@@ -14,285 +14,323 @@ ALU = mybir.AluOpType
 
 P = 128
 B, IN, OUT, ORDERS = 1024, 512, 512, 10
+TILES = B // P
 FLOPS = 2 * B * OUT * (IN * ORDERS + IN)
-Q = 104
+CLASSES = 10
+SLOTS = 104
+HALVES = ((0, 52), (52, 104))
 QUARTERS = ((0, 26), (26, 52), (52, 78), (78, 104))
-SPLITQ = {5: (52,)}
-SCALAR_FINALS = ((6, 4), (8, 6), (8, 7))
-MANUAL = True
-ORDER = (
-    ("ldx", 0), ("ldx", 1), ("xsp", 0), ("ldx", 2), ("xsp", 1), ("xev", 0),
-    ("ldx", 3), ("xsp", 2), ("xev", 1), ("ldw", 0), ("xsp", 3), ("xev", 2),
-    ("y", 0, 1), ("F", 1, 0), ("F", 1, 1), ("xev", 3), ("y", 1, 2), ("Qz", 0, 0, 8),
-    ("ldw", 1), ("wt", 0, 0), ("y", 2, 3), ("Qz", 0, 8, 2), ("T3", 0, 2), ("wt", 0, 1),
-    ("y", 3, 4), ("wt", 0, 2), ("wt", 0, 3), ("ldw", 2), ("wev", 0, 0), ("wt", 1, 0),
-    ("F", 1, 2), ("wev", 0, 1), ("F", 1, 3), ("wt", 1, 1), ("wev", 0, 2), ("T3", 2, 4),
-    ("wt", 1, 2), ("wev", 0, 3), ("wt", 1, 3), ("ldw", 3), ("wev", 1, 0), ("wt", 2, 0),
-    ("wev", 1, 1), ("wt", 2, 1), ("qw", 0), ("wev", 1, 2), ("wt", 2, 2), ("wev", 1, 3),
-    ("F", 2, 0), ("wt", 2, 3), ("ldw", 4), ("wev", 2, 0), ("wt", 3, 0), ("F", 2, 1),
-    ("wev", 2, 1), ("qw", 1), ("wt", 3, 1), ("wev", 2, 2), ("wt", 3, 2), ("Qz", 1, 0, 8),
-    ("wev", 2, 3), ("wt", 3, 3), ("ldW",), ("s4", 2, 4), ("wt", 4, 0), ("Qz", 1, 8, 2),
-    ("qw", 2), ("wt", 4, 1), ("F", 2, 2), ("wev", 3, 0), ("F", 2, 3), ("wev", 3, 1),
-    ("wt", 4, 2), ("F", 3, 2), ("F", 3, 3), ("wev", 3, 2), ("wt", 4, 3), ("F", 3, 0),
-    ("F", 3, 1), ("wev", 3, 3), ("xsi", 0), ("s4", 0, 2), ("qw", 3), ("xsi", 1),
-    ("Qz", 2, 0, 8), ("wev", 4, 0), ("Qz", 2, 8, 2), ("wev", 4, 1), ("xsi", 2), ("F", 4, 0),
-    ("wev", 4, 2), ("xsi", 3), ("wev", 4, 3), ("F", 4, 1), ("q5", 0, 2), ("mm", 1, 0, 8),
-    ("qw", 4), ("Qz", 3, 0, 8), ("q5", 2, 4), ("Qz", 3, 8, 2), ("F", 5, 0), ("mm", 1, 8, 2),
-    ("mm", 0, 0, 8), ("s6", 2, 4), ("F", 5, 1), ("mm", 0, 8, 2), ("s6", 0, 2), ("t7", 0, 2),
-    ("silu", 0), ("F", 6, 2), ("silu", 1), ("mm", 3, 0, 8), ("F", 6, 3), ("silu", 2),
-    ("t7", 2, 4), ("silu", 3), ("F", 7, 0), ("mm", 3, 8, 2), ("F", 6, 0), ("mm", 2, 0, 8),
-    ("F", 6, 1), ("s8", 0, 2), ("F", 7, 1), ("qsilu",), ("mm", 2, 8, 2), ("Qz", 4, 0, 8),
-    ("mb", 0), ("s8", 2, 4), ("mb", 1), ("Qz", 4, 8, 2), ("mm", 4, 0, 8), ("Qz", 5, 0, 8),
-    ("F", 8, 2), ("Qz", 5, 8, 2), ("F", 8, 3), ("F", 7, 2), ("mm", 4, 8, 2), ("bev", 0),
-    ("bev", 1), ("mb", 2), ("F", 7, 3), ("F", 9, 0), ("F", 8, 0), ("mb", 3),
-    ("mm", 5, 0, 8), ("F", 8, 1), ("epi", 0), ("mm", 5, 8, 2), ("epi", 1), ("st", 0),
-    ("bev", 2), ("Qz", 6, 0, 8), ("st", 1), ("bev", 3), ("mb", 4), ("bev", 4),
-    ("mb", 5), ("Qz", 6, 8, 2), ("mm", 6, 0, 8), ("Qz", 7, 0, 4), ("bev", 5), ("Qz", 7, 4, 2),
-    ("F", 9, 1), ("mm", 6, 8, 2), ("mm", 7, 0, 4), ("epi", 2), ("epi", 3), ("st", 2),
-    ("mm", 7, 4, 2), ("Qz", 7, 6, 4), ("st", 3), ("mb", 6), ("epi", 4), ("mb", 7),
-    ("bev", 6), ("mm", 7, 6, 4), ("epi", 5), ("st", 4), ("bev", 7), ("epi", 6),
-    ("st", 5), ("epi", 7), ("st", 6), ("st", 7),
-)
 
 
-def final_segments(n):
+def runs_of_order(n, cut=None):
     exact = n in (4, 9)
-    cuts = SPLITQ.get(n, ())
-    rows = []
-    for rho in range(10):
-        r0 = B * n + rho
-        c, m0 = r0 % 10, r0 // 10
-        cnt = (103 if rho < 4 else 102) if exact else Q
+    pieces = []
+    for rho in range(CLASSES):
+        c, m = (B * n + rho) % 10, (B * n + rho) // 10
+        count = (103 if rho < 4 else 102) if exact else SLOTS
         q = 0
-        while q < cnt:
-            mu, ml = divmod(m0 + q, P)
-            take = min([cnt - q, P - ml] + [k - q for k in cuts if k > q])
-            rows.append((mu, q, take, ml, rho, c))
+        while q < count:
+            tile_index, column = divmod(m + q, P)
+            take = min(count - q, P - column)
+            if cut is not None and q < cut:
+                take = min(take, cut - q)
+            pieces.append((tile_index, q, take, column, rho, c))
             q += take
-    segs = []
-    for mu, q, take, ml, rho, c in sorted(rows):
-        if segs:
-            last = segs[-1]
-            if last[:4] == [mu, q, take, ml] and last[4] + last[6] == rho and last[5] + last[6] == c:
+    runs = []
+    for tile_index, q, take, column, rho, c in sorted(pieces):
+        if runs:
+            last = runs[-1]
+            if last[:4] == [tile_index, q, take, column] and last[4] + last[6] == rho and last[5] + last[6] == c:
                 last[6] += 1
                 continue
-        segs.append([mu, q, take, ml, rho, c, 1])
-    return segs
+        runs.append([tile_index, q, take, column, rho, c, 1])
+    return runs
 
 
 def tile_kantlinear_kernel(tc, x, base_weight_words, base_weight_scales, cheby_weight, out):
     nc = tc.nc
     with ExitStack() as ctx:
         keep = ctx.enter_context(tc.tile_pool(name="keep", bufs=1))
-        xrp = ctx.enter_context(tc.tile_pool(name="xrp", bufs=4))
-        wrp = ctx.enter_context(tc.tile_pool(name="wrp", bufs=3))
-        gwp = ctx.enter_context(tc.tile_pool(name="gwp", bufs=2))
-        gfp = ctx.enter_context(tc.tile_pool(name="gfp", bufs=3))
-        cfp = ctx.enter_context(tc.tile_pool(name="cfp", bufs=5))
-        epi = ctx.enter_context(tc.tile_pool(name="epi", bufs=6))
-        psp = ctx.enter_context(tc.psum_pool(name="psp", bufs=6))
-        bpp = ctx.enter_context(tc.psum_pool(name="bpp", bufs=2))
-        if MANUAL:
-            ctx.enter_context(tc.manual_schedule())
+        x_pool = ctx.enter_context(tc.tile_pool(name="x_rows", bufs=4))
+        w_pool = ctx.enter_context(tc.tile_pool(name="w_rows", bufs=3))
+        wg_pool = ctx.enter_context(tc.tile_pool(name="w_grouped", bufs=2))
+        flat_pool = ctx.enter_context(tc.tile_pool(name="flat", bufs=3))
+        code_pool = ctx.enter_context(tc.tile_pool(name="flat_codes", bufs=5))
+        out_pool = ctx.enter_context(tc.tile_pool(name="out_rows", bufs=6))
+        bank_pool = ctx.enter_context(tc.psum_pool(name="banks", bufs=6))
+        base_pool = ctx.enter_context(tc.psum_pool(name="base_banks", bufs=2))
+        ctx.enter_context(tc.manual_schedule())
 
-        ident = keep.tile([P, P], F32, name="ident")
-        xs = keep.tile([P, 10, Q, 4], BF16, name="xs", align_bytes=64)
-        gs = keep.tile([P, B, 2, 2], BF16, name="gs", align_bytes=64)
-        cs = keep.tile([P, B], U32, name="cs", align_bytes=64)
-        ss = keep.tile([P, B], U8, name="ss", align_bytes=64)
-        ww = keep.tile([P, OUT], U32, name="ww", align_bytes=64)
-        ws = keep.tile([P, OUT], U8, name="ws", align_bytes=64)
-        cw = keep.tile([P, ORDERS, OUT], U32, name="cw", align_bytes=64)
-        sw = keep.tile([P, ORDERS, OUT], U8, name="sw", align_bytes=64)
-        ta = keep.tile([P, 10, Q, 4], F32, name="ta")
-        tb = keep.tile([P, 10, Q, 4], F32, name="tb")
-        t3 = keep.tile([P, 10, Q, 4], F32, name="t3")
-        td = keep.tile([P, 10, Q, 4], F32, name="td")
-        xsw = xs[:].bitcast(F32)
-        wv = cheby_weight.rearrange("o i k -> o (i k)")
+        identity = keep.tile([P, P], F32, name="identity")
+        xs = keep.tile([P, CLASSES, SLOTS, 4], BF16, name="xs", align_bytes=64)
+        silu_bf = keep.tile([P, B, 2, 2], BF16, name="silu_bf", align_bytes=64)
+        silu_codes = keep.tile([P, B], U32, name="silu_codes", align_bytes=64)
+        silu_scales = keep.tile([P, B], U8, name="silu_scales", align_bytes=64)
+        base_codes = keep.tile([P, OUT], U32, name="base_codes", align_bytes=64)
+        base_scales = keep.tile([P, OUT], U8, name="base_scales", align_bytes=64)
+        w_codes = keep.tile([P, ORDERS, OUT], U32, name="w_codes", align_bytes=64)
+        w_scales = keep.tile([P, ORDERS, OUT], U8, name="w_scales", align_bytes=64)
+        buf_y = keep.tile([P, CLASSES, SLOTS, 4], F32, name="buf_y")
+        buf_4 = keep.tile([P, CLASSES, SLOTS, 4], F32, name="buf_4")
+        buf_3 = keep.tile([P, CLASSES, SLOTS, 4], F32, name="buf_3")
+        buf_6 = keep.tile([P, CLASSES, SLOTS, 4], F32, name="buf_6")
+        xs_words = xs[:].bitcast(F32)
+        w_flat = cheby_weight.rearrange("o i k -> o (i k)")
 
-        make_identity(nc, ident[:])
-        nc.vector.memset(xsw[:, :, 102:104, :], 0.0)
-        nc.vector.memset(ws[:].bitcast(I32), 0)
+        x_rows, x_banks, silu_banks = {}, {}, {}
+        w_rows, w_banks, w_grouped = {}, {}, {}
+        flat, flat_codes, flat_scales = {}, {}, {}
+        sums, base_sums, rows_out, passes_done = {}, {}, {}, {}
 
-        live = {}
+        def bank(name):
+            return bank_pool.tile([P, 2, 256], F32, name=name, tag="bank")
 
-        def get(kind, i, make):
-            if (kind, i) not in live:
-                live[(kind, i)] = make()
-            return live[(kind, i)]
+        def flat_tile(mu):
+            if mu not in flat:
+                flat[mu] = flat_pool.tile([P, ORDERS, P, 4], BF16, name="flat%d" % mu, tag="flat", align_bytes=64)
+            return flat[mu]
 
-        def gf_tile(mu):
-            return get("gf", mu, lambda: gfp.tile([P, 10, P, 4], BF16, name="gf%d" % mu, tag="gf", align_bytes=64))
+        def load_x(k):
+            x_rows[k] = x_pool.tile([P, 2, IN], BF16, name="x_rows%d" % k, tag="x_rows")
+            nc.sync.dma_start(out=x_rows[k][:], in_=x[256 * k:256 * k + 256, :].rearrange("(a p) i -> p a i", p=P))
 
-        def cf_tile(mu):
-            return get("cf", mu, lambda: cfp.tile([P, 10 * P], U32, name="cf%d" % mu, tag="cf", align_bytes=64))
+        def load_w(g):
+            w_rows[g] = w_pool.tile([P, 4, 1024], BF16, name="w_rows%d" % g, tag="w_rows")
+            nc.sync.dma_start(out=w_rows[g][:],
+                              in_=w_flat[:, 1024 * g:1024 * g + 1024].rearrange("(h p) j -> p h j", p=P))
 
-        def sf_tile(mu):
-            return get("sf", mu, lambda: cfp.tile([P, 10 * P], U8, name="sf%d" % mu, tag="sf", align_bytes=64))
-
-        def ps_tile(kind, i):
-            return get(kind, i, lambda: psp.tile([P, 2, 256], F32, name="%s%d" % (kind, i), tag="ps"))
-
-        nc.vector.memset(gf_tile(0)[:], 1.0)
-
-        def ldx(k):
-            t = get("xr", k, lambda: xrp.tile([P, 2, IN], BF16, name="xr%d" % k, tag="xr"))
-            nc.sync.dma_start(out=t[:], in_=x[256 * k:256 * k + 256, :].rearrange("(a p) i -> p a i", p=P))
-
-        def ldw(g):
-            t = get("wr", g, lambda: wrp.tile([P, 4, 1024], BF16, name="wr%d" % g, tag="wr"))
-            nc.sync.dma_start(out=t[:], in_=wv[:, 1024 * g:1024 * g + 1024].rearrange("(h p) j -> p h j", p=P))
-
-        def ldbase():
-            nc.sync.dma_start(out=ww[:].bitcast(I32),
+        def load_base_weight():
+            nc.sync.dma_start(out=base_codes[:].bitcast(I32),
                               in_=base_weight_words[0].rearrange("p n t -> p (n t)").bitcast(I32))
-            for qd in range(4):
-                nc.sync.dma_start(out=ws[32 * qd:32 * qd + 4, :].bitcast(I32),
-                                  in_=base_weight_scales[0, 4 * qd:4 * qd + 4, :].bitcast(I32))
+            for quadrant in range(4):
+                nc.sync.dma_start(out=base_scales[32 * quadrant:32 * quadrant + 4, :].bitcast(I32),
+                                  in_=base_weight_scales[0, 4 * quadrant:4 * quadrant + 4, :].bitcast(I32))
 
-        def xsp(k):
-            tp = ps_tile("tpx", k)
+        def transpose_x(k):
+            x_banks[k] = bank("x_bank%d" % k)
             for a in range(2):
-                xw = live[("xr", k)][:, a, :].bitcast(F32)
+                words = x_rows[k][:, a, :].bitcast(F32)
                 for u in range(2):
-                    nc.tensor.transpose(tp[:, u, P * a:P * a + P], xw[:, P * u:P * u + P], ident[:])
+                    nc.tensor.transpose(x_banks[k][:, u, P * a:P * a + P], words[:, P * u:P * u + P], identity[:])
 
-        def xev(k):
-            tp = live[("tpx", k)]
-            b0 = 256 * k
-            q_lo = -(-b0 // 10)
-            q_hi = (b0 + 256) // 10
-            head = 10 * q_lo - b0
-            tail = b0 + 256 - 10 * q_hi
-            nc.vector.tensor_copy(out=xsw[:, :, q_lo:q_hi, :],
-                                  in_=tp[:, :, head:head + 10 * (q_hi - q_lo)].rearrange("p u (q r) -> p r q u", r=10))
+        def sort_x(k):
+            first = 256 * k
+            q_lo, q_hi = -(-first // 10), (first + 256) // 10
+            head, tail = 10 * q_lo - first, first + 256 - 10 * q_hi
+            nc.vector.tensor_copy(
+                out=xs_words[:, :, q_lo:q_hi, :],
+                in_=x_banks[k][:, :, head:head + 10 * (q_hi - q_lo)].rearrange("p u (q r) -> p r q u", r=10))
             if head:
-                nc.vector.tensor_copy(out=xsw[:, 10 - head:10, q_lo - 1, :],
-                                      in_=tp[:, :, 0:head].rearrange("p u r -> p r u"))
+                nc.vector.tensor_copy(out=xs_words[:, 10 - head:10, q_lo - 1, :],
+                                      in_=x_banks[k][:, :, 0:head].rearrange("p u r -> p r u"))
             if tail:
-                nc.vector.tensor_copy(out=xsw[:, 0:tail, q_hi, :],
-                                      in_=tp[:, :, 256 - tail:256].rearrange("p u r -> p r u"))
+                nc.vector.tensor_copy(out=xs_words[:, 0:tail, q_hi, :],
+                                      in_=x_banks[k][:, :, 256 - tail:256].rearrange("p u r -> p r u"))
 
-        def xsi(k):
-            tp = ps_tile("tps", k)
+        def transpose_x_for_silu(k):
+            silu_banks[k] = bank("silu_bank%d" % k)
             for a in range(2):
-                xw = live[("xr", k)][:, a, :].bitcast(F32)
+                words = x_rows[k][:, a, :].bitcast(F32)
                 for u in range(2):
-                    nc.tensor.transpose(tp[:, u, P * a:P * a + P], xw[:, u:256:2], ident[:])
+                    nc.tensor.transpose(silu_banks[k][:, u, P * a:P * a + P], words[:, u:256:2], identity[:])
 
         def silu(k):
-            nc.scalar.activation(out=gs[:, 256 * k:256 * k + 256, :, :],
-                                 in_=live[("tps", k)][:].bitcast(BF16).rearrange("p u (b e) -> p b u e", e=2),
+            nc.scalar.activation(out=silu_bf[:, 256 * k:256 * k + 256, :, :],
+                                 in_=silu_banks[k][:].bitcast(BF16).rearrange("p u (b e) -> p b u e", e=2),
                                  func=ACT.Silu)
 
-        def qsilu():
-            nc.vector.quantize_mx(out=cs[:].bitcast(FP8X4), scales=ss[:], in_=gs[:].rearrange("p b u e -> p (b u e)"))
+        def quantise_silu():
+            nc.vector.quantize_mx(out=silu_codes[:].bitcast(FP8X4), scales=silu_scales[:],
+                                  in_=silu_bf[:].rearrange("p b u e -> p (b u e)"))
 
-        def wt(g, h):
-            cc, hb = divmod(h, 2)
-            tp = ps_tile("tpw", 4 * g + h)
-            for a in range(2):
-                src = live[("wr", g)][:, 2 * hb + a, :].bitcast(F32)
-                for u in range(2):
-                    lo = 256 * cc + P * u
-                    nc.tensor.transpose(tp[:, u, P * a:P * a + P], src[:, lo:lo + P], ident[:])
+        def transpose_w(g):
+            for h in range(4):
+                w_banks[g, h] = bank("w_bank%d_%d" % (g, h))
+                for a in range(2):
+                    words = w_rows[g][:, 2 * (h % 2) + a, :].bitcast(F32)
+                    for u in range(2):
+                        low = 256 * (h // 2) + P * u
+                        nc.tensor.transpose(w_banks[g, h][:, u, P * a:P * a + P], words[:, low:low + P], identity[:])
 
-        def wev(g, h):
-            cc, hb = divmod(h, 2)
-            gw = get("gw", g, lambda: gwp.tile([P, 2, OUT, 4], BF16, name="gw%d" % g, tag="gw", align_bytes=64))
-            nc.scalar.copy(out=gw[:].bitcast(F32)[:, cc, 256 * hb:256 * hb + 256, :],
-                           in_=live[("tpw", 4 * g + h)][:].rearrange("p u o -> p o u"))
+        def group_w(g):
+            w_grouped[g] = wg_pool.tile([P, 2, OUT, 4], BF16, name="w_grouped%d" % g, tag="w_grouped", align_bytes=64)
+            for h in range(4):
+                nc.scalar.copy(out=w_grouped[g][:].bitcast(F32)[:, h // 2, 256 * (h % 2):256 * (h % 2) + 256, :],
+                               in_=w_banks[g, h][:].rearrange("p u o -> p o u"))
 
-        def qw(g):
-            nc.vector.quantize_mx(out=cw[:, 2 * g:2 * g + 2, :].rearrange("p c o -> p (c o)").bitcast(FP8X4),
-                                  scales=sw[:, 2 * g:2 * g + 2, :].rearrange("p c o -> p (c o)"),
-                                  in_=live[("gw", g)][:].rearrange("p c o t -> p (c o t)"))
+        def quantise_w(g):
+            nc.vector.quantize_mx(out=w_codes[:, 2 * g:2 * g + 2, :].rearrange("p c o -> p (c o)").bitcast(FP8X4),
+                                  scales=w_scales[:, 2 * g:2 * g + 2, :].rearrange("p c o -> p (c o)"),
+                                  in_=w_grouped[g][:].rearrange("p c o t -> p (c o t)"))
 
-        def square(dst, src, scale, bias):
-            def run(j0, j1):
-                q0, q1 = QUARTERS[j0][0], QUARTERS[j1 - 1][1]
-                nc.scalar.activation(out=dst[:, :, q0:q1, :], in_=src[:, :, q0:q1, :], func=ACT.Square,
-                                     bias=bias, scale=scale)
-            return run
+        def square(dst, src, scale, bias, slots):
+            nc.scalar.activation(out=dst[:, :, slots[0]:slots[1], :], in_=src[:, :, slots[0]:slots[1], :],
+                                 func=ACT.Square, bias=bias, scale=scale)
 
-        def product(dst, in0, shift, in1):
-            def run(j0, j1):
-                q0, q1 = QUARTERS[j0][0], QUARTERS[j1 - 1][1]
-                nc.vector.scalar_tensor_tensor(out=dst[:, :, q0:q1, :], in0=in0[:, :, q0:q1, :], scalar=shift,
-                                               in1=in1[:, :, q0:q1, :], op0=ALU.add, op1=ALU.mult)
-            return run
+        def shifted_product(dst, in0, shift, in1, slots):
+            nc.vector.scalar_tensor_tensor(out=dst[:, :, slots[0]:slots[1], :], in0=in0[:, :, slots[0]:slots[1], :],
+                                           scalar=shift, in1=in1[:, :, slots[0]:slots[1], :],
+                                           op0=ALU.add, op1=ALU.mult)
 
-        def affine(src):
-            def run(n, dst, sl):
-                if n in SCALAR_FINALS:
-                    nc.scalar.activation(out=dst, in_=sl(src), func=ACT.Copy, bias=-1.0, scale=0.5)
-                else:
-                    nc.vector.tensor_scalar(out=dst, in0=sl(src), scalar1=0.5, scalar2=-1.0, op0=ALU.mult, op1=ALU.add)
-            return run
+        def place(n, emit, tiles=None, cut=None):
+            for mu, q, count, column, rho, c, classes in runs_of_order(n, cut):
+                if tiles is None or mu in tiles:
+                    emit(flat_tile(mu)[:, c:c + classes, column:column + count, :],
+                         lambda t: t[:, rho:rho + classes, q:q + count, :])
 
-        def shifted_product(in0, shift, in1):
-            return lambda n, dst, sl: nc.vector.scalar_tensor_tensor(out=dst, in0=sl(in0), scalar=shift, in1=sl(in1),
-                                                                     op0=ALU.add, op1=ALU.mult)
+        def copy_of(src):
+            return lambda dst, part: nc.vector.tensor_copy(out=dst, in_=part(src))
 
-        emitters = {
-            1: lambda n, dst, sl: nc.vector.tensor_copy(out=dst, in_=sl(xs)),
-            2: affine(ta),
-            3: lambda n, dst, sl: nc.vector.tensor_copy(out=dst, in_=sl(t3)),
-            4: affine(tb),
-            5: shifted_product(ta, -1.25, xs),
-            6: affine(td),
-            7: lambda n, dst, sl: nc.vector.tensor_tensor(out=dst, in0=sl(ta), in1=sl(xs), op=ALU.subtract),
-            8: affine(tb),
-            9: shifted_product(td, -3.0, t3),
-        }
+        def half_minus_one(src):
+            return lambda dst, part: nc.vector.tensor_scalar(out=dst, in0=part(src), scalar1=0.5, scalar2=-1.0,
+                                                             op0=ALU.mult, op1=ALU.add)
 
-        def final(n, i):
-            mu, q, take, ml, rho, c, nr = final_segments(n)[i]
-            emitters[n]((n, mu), gf_tile(mu)[:, c:c + nr, ml:ml + take, :], lambda t: t[:, rho:rho + nr, q:q + take, :])
+        def half_minus_one_on_scalar(src):
+            return lambda dst, part: nc.scalar.activation(out=dst, in_=part(src), func=ACT.Copy, bias=-1.0, scale=0.5)
 
-        def quantise_flat(mu, c0, ncs):
-            nc.vector.quantize_mx(
-                out=cf_tile(mu)[:, P * c0:P * (c0 + ncs)].bitcast(FP8X4),
-                scales=sf_tile(mu)[:, P * c0:P * (c0 + ncs)],
-                in_=gf_tile(mu)[:, c0:c0 + ncs, :, :].rearrange("p c m t -> p (c m t)"))
+        def product_of(in0, shift, in1):
+            return lambda dst, part: nc.vector.scalar_tensor_tensor(out=dst, in0=part(in0), scalar=shift, in1=part(in1),
+                                                                    op0=ALU.add, op1=ALU.mult)
 
-        done = {}
+        def difference_of(in0, in1):
+            return lambda dst, part: nc.vector.tensor_tensor(out=dst, in0=part(in0), in1=part(in1), op=ALU.subtract)
 
-        def mm(mu, c0, ncs):
-            acc = ps_tile("acc", mu)
-            for c in range(c0, c0 + ncs):
-                done[mu] = done.get(mu, 0) + 1
-                nc.tensor.matmul_mx(out=acc[:].rearrange("p a b -> p (a b)"),
-                                    lhsT=cf_tile(mu)[:, P * c:P * c + P].bitcast(FP8X4),
-                                    lhsT_scale=sf_tile(mu)[:, P * c:P * c + P],
-                                    rhs=cw[:, c, :].bitcast(FP8X4), rhs_scale=sw[:, c, :],
-                                    start=(done[mu] == 1), stop=(done[mu] == ORDERS))
+        def quantise_flat(mu, pieces=((0, 8), (8, 2))):
+            if mu not in flat_codes:
+                flat_codes[mu] = code_pool.tile([P, ORDERS * P], U32, name="flat_codes%d" % mu, tag="codes", align_bytes=64)
+                flat_scales[mu] = code_pool.tile([P, ORDERS * P], U8, name="flat_scales%d" % mu, tag="scales",
+                                                 align_bytes=64)
+            for c, count in pieces:
+                nc.vector.quantize_mx(out=flat_codes[mu][:, P * c:P * (c + count)].bitcast(FP8X4),
+                                      scales=flat_scales[mu][:, P * c:P * (c + count)],
+                                      in_=flat[mu][:, c:c + count, :, :].rearrange("p c m t -> p (c m t)"))
 
-        def mb(mu):
-            bp = get("bp", mu, lambda: bpp.tile([P, OUT], F32, name="bp%d" % mu, tag="bp"))
-            nc.tensor.matmul_mx(out=bp[:], lhsT=cs[:, P * mu:P * mu + P].bitcast(FP8X4),
-                                lhsT_scale=ss[:, P * mu:P * mu + P],
-                                rhs=ww[:].bitcast(FP8X4), rhs_scale=ws[:], start=True, stop=True)
+        def spline_passes(mu, first=0, count=ORDERS):
+            if mu not in sums:
+                sums[mu] = bank("sum%d" % mu)
+            for c in range(first, first + count):
+                passes_done[mu] = passes_done.get(mu, 0) + 1
+                nc.tensor.matmul_mx(out=sums[mu][:].rearrange("p a b -> p (a b)"),
+                                    lhsT=flat_codes[mu][:, P * c:P * c + P].bitcast(FP8X4),
+                                    lhsT_scale=flat_scales[mu][:, P * c:P * c + P],
+                                    rhs=w_codes[:, c, :].bitcast(FP8X4), rhs_scale=w_scales[:, c, :],
+                                    start=(passes_done[mu] == 1), stop=(passes_done[mu] == ORDERS))
 
-        def bev(mu):
-            bs = get("bs", mu, lambda: epi.tile([P, OUT], F32, name="bs%d" % mu, tag="bs"))
-            nc.scalar.copy(out=bs[:], in_=live[("bp", mu)][:])
+        def base_pass(mu):
+            base_sums[mu] = base_pool.tile([P, OUT], F32, name="base_sum%d" % mu, tag="base_sum")
+            nc.tensor.matmul_mx(out=base_sums[mu][:], lhsT=silu_codes[:, P * mu:P * mu + P].bitcast(FP8X4),
+                                lhsT_scale=silu_scales[:, P * mu:P * mu + P],
+                                rhs=base_codes[:].bitcast(FP8X4), rhs_scale=base_scales[:], start=True, stop=True)
 
-        def epilogue(mu):
-            nc.vector.scalar_tensor_tensor(out=live[("bs", mu)][:], in0=live[("acc", mu)][:].rearrange("p a b -> p (a b)"), scalar=0.1,
-                                           in1=live[("bs", mu)][:], op0=ALU.mult, op1=ALU.add)
+        def base_out(mu):
+            rows_out[mu] = out_pool.tile([P, OUT], F32, name="rows_out%d" % mu, tag="rows_out")
+            nc.scalar.copy(out=rows_out[mu][:], in_=base_sums[mu][:])
 
-        def store(mu):
-            nc.sync.dma_start(out=out[P * mu:P * mu + P, :], in_=live[("bs", mu)][:])
+        def finish(mu):
+            nc.vector.scalar_tensor_tensor(out=rows_out[mu][:], in0=sums[mu][:].rearrange("p a b -> p (a b)"), scalar=0.1,
+                                           in1=rows_out[mu][:], op0=ALU.mult, op1=ALU.add)
+            nc.sync.dma_start(out=out[P * mu:P * mu + P, :], in_=rows_out[mu][:])
 
-        steps = {
-            "ldx": ldx, "ldw": ldw, "ldW": ldbase, "xsp": xsp, "xev": xev, "xsi": xsi, "silu": silu, "qsilu": qsilu,
-            "wt": wt, "wev": wev, "qw": qw,
-            "y": square(ta, xs, 2.0, 0.0), "s4": square(tb, ta, 1.0, -2.0), "q5": square(ta, ta, 1.0, -2.5),
-            "s6": square(td, t3, 2.0, 0.0), "s8": square(tb, tb, 1.0, -2.0),
-            "T3": product(t3, ta, -3.0, xs), "t7": product(ta, tb, -2.0, t3),
-            "F": final, "Qz": quantise_flat, "mm": mm, "mb": mb, "bev": bev, "epi": epilogue, "st": store,
-        }
-        for name in ORDER:
-            steps[name[0]](*name[1:])
+        make_identity(nc, identity[:])
+        nc.vector.memset(xs_words[:, :, 102:SLOTS, :], 0.0)
+        nc.vector.memset(base_scales[:].bitcast(I32), 0)
+        nc.vector.memset(flat_tile(0)[:], 1.0)
+        for k in range(4):
+            load_x(k)
+        for g in range(3):
+            load_w(g)
+
+        for k in range(4):
+            transpose_x(k)
+            sort_x(k)
+        for slots in QUARTERS:
+            square(buf_y, xs, 2.0, 0.0, slots)
+        place(1, copy_of(xs))
+        quantise_flat(0)
+        for slots in HALVES:
+            shifted_product(buf_3, buf_y, -3.0, xs, slots)
+
+        for g in range(5):
+            transpose_w(g)
+            if g + 3 < 5:
+                load_w(g + 3)
+            if g == 1:
+                load_base_weight()
+            group_w(g)
+            quantise_w(g)
+            if g == 0:
+                place(2, half_minus_one(buf_y))
+            elif g == 1:
+                quantise_flat(1)
+            elif g == 2:
+                square(buf_4, buf_y, 1.0, -2.0, HALVES[0])
+                place(3, copy_of(buf_3))
+            elif g == 3:
+                square(buf_4, buf_y, 1.0, -2.0, HALVES[1])
+                quantise_flat(2)
+                place(4, half_minus_one(buf_4))
+            else:
+                quantise_flat(3)
+
+        for k in range(4):
+            transpose_x_for_silu(k)
+        for mu in range(4):
+            spline_passes(mu)
+
+        for slots in HALVES:
+            square(buf_y, buf_y, 1.0, -2.5, slots)
+        for slots in HALVES:
+            square(buf_6, buf_3, 2.0, 0.0, slots)
+        for k in range(4):
+            silu(k)
+        place(5, product_of(buf_y, -1.25, xs), cut=HALVES[0][1])
+        shifted_product(buf_y, buf_4, -2.0, buf_3, HALVES[0])
+        place(6, half_minus_one_on_scalar(buf_6), tiles=(4,))
+        place(6, half_minus_one(buf_6), tiles=(5,))
+        shifted_product(buf_y, buf_4, -2.0, buf_3, HALVES[1])
+        for slots in HALVES:
+            square(buf_4, buf_4, 1.0, -2.0, slots)
+        place(7, difference_of(buf_y, xs), tiles=(5,))
+        quantise_silu()
+        base_pass(0)
+        base_pass(1)
+        quantise_flat(4)
+        spline_passes(4)
+        base_pass(2)
+        base_pass(3)
+        quantise_flat(5)
+        spline_passes(5)
+        base_pass(4)
+        base_pass(5)
+        place(7, difference_of(buf_y, xs), tiles=(6,))
+        place(8, half_minus_one_on_scalar(buf_4), tiles=(7,))
+        base_out(0)
+        base_out(1)
+        place(8, half_minus_one_on_scalar(buf_4), tiles=(6,))
+
+        ninth = runs_of_order(9)
+        place_ninth = product_of(buf_6, -3.0, buf_3)
+
+        def place_run(run):
+            mu, q, count, column, rho, c, classes = run
+            place_ninth(flat_tile(mu)[:, c:c + classes, column:column + count, :],
+                        lambda t: t[:, rho:rho + classes, q:q + count, :])
+
+        place_run(ninth[0])
+        finish(0)
+        finish(1)
+        quantise_flat(6)
+        spline_passes(6)
+        quantise_flat(7, ((0, 4), (4, 2)))
+        spline_passes(7, 0, 6)
+        base_pass(6)
+        base_pass(7)
+        for mu in range(2, TILES):
+            base_out(mu)
+        place_run(ninth[1])
+        finish(2)
+        finish(3)
+        quantise_flat(7, ((6, 4),))
+        spline_passes(7, 6, 4)
+        for mu in range(4, TILES):
+            finish(mu)

from contextlib import ExitStack

import concourse.mybir as mybir
from concourse.masks import make_identity

F32 = mybir.dt.float32
BF16 = mybir.dt.bfloat16
U32 = mybir.dt.uint32
U8 = mybir.dt.uint8
I32 = mybir.dt.int32
FP8X4 = mybir.dt.float8_e4m3fn_x4
ACT = mybir.ActivationFunctionType
ALU = mybir.AluOpType

P = 128
B, IN, OUT, ORDERS = 1024, 512, 512, 10
TILES = B // P
FLOPS = 2 * B * OUT * (IN * ORDERS + IN)
CLASSES = 10
SLOTS = 104
HALVES = ((0, 52), (52, 104))
QUARTERS = ((0, 26), (26, 52), (52, 78), (78, 104))


def runs_of_order(n, cut=None):
    exact = n in (4, 9)
    pieces = []
    for rho in range(CLASSES):
        c, m = (B * n + rho) % 10, (B * n + rho) // 10
        count = (103 if rho < 4 else 102) if exact else SLOTS
        q = 0
        while q < count:
            tile_index, column = divmod(m + q, P)
            take = min(count - q, P - column)
            if cut is not None and q < cut:
                take = min(take, cut - q)
            pieces.append((tile_index, q, take, column, rho, c))
            q += take
    runs = []
    for tile_index, q, take, column, rho, c in sorted(pieces):
        if runs:
            last = runs[-1]
            if last[:4] == [tile_index, q, take, column] and last[4] + last[6] == rho and last[5] + last[6] == c:
                last[6] += 1
                continue
        runs.append([tile_index, q, take, column, rho, c, 1])
    return runs


def tile_kantlinear_kernel(tc, x, base_weight_words, base_weight_scales, cheby_weight, out):
    nc = tc.nc
    with ExitStack() as ctx:
        keep = ctx.enter_context(tc.tile_pool(name="keep", bufs=1))
        x_pool = ctx.enter_context(tc.tile_pool(name="x_rows", bufs=4))
        w_pool = ctx.enter_context(tc.tile_pool(name="w_rows", bufs=3))
        wg_pool = ctx.enter_context(tc.tile_pool(name="w_grouped", bufs=2))
        flat_pool = ctx.enter_context(tc.tile_pool(name="flat", bufs=3))
        code_pool = ctx.enter_context(tc.tile_pool(name="flat_codes", bufs=5))
        out_pool = ctx.enter_context(tc.tile_pool(name="out_rows", bufs=6))
        bank_pool = ctx.enter_context(tc.psum_pool(name="banks", bufs=6))
        base_pool = ctx.enter_context(tc.psum_pool(name="base_banks", bufs=2))
        ctx.enter_context(tc.manual_schedule())

        identity = keep.tile([P, P], F32, name="identity")
        xs = keep.tile([P, CLASSES, SLOTS, 4], BF16, name="xs", align_bytes=64)
        silu_bf = keep.tile([P, B, 2, 2], BF16, name="silu_bf", align_bytes=64)
        silu_codes = keep.tile([P, B], U32, name="silu_codes", align_bytes=64)
        silu_scales = keep.tile([P, B], U8, name="silu_scales", align_bytes=64)
        base_codes = keep.tile([P, OUT], U32, name="base_codes", align_bytes=64)
        base_scales = keep.tile([P, OUT], U8, name="base_scales", align_bytes=64)
        w_codes = keep.tile([P, ORDERS, OUT], U32, name="w_codes", align_bytes=64)
        w_scales = keep.tile([P, ORDERS, OUT], U8, name="w_scales", align_bytes=64)
        buf_y = keep.tile([P, CLASSES, SLOTS, 4], F32, name="buf_y")
        buf_4 = keep.tile([P, CLASSES, SLOTS, 4], F32, name="buf_4")
        buf_3 = keep.tile([P, CLASSES, SLOTS, 4], F32, name="buf_3")
        buf_6 = keep.tile([P, CLASSES, SLOTS, 4], F32, name="buf_6")
        xs_words = xs[:].bitcast(F32)
        w_flat = cheby_weight.rearrange("o i k -> o (i k)")

        x_rows, x_banks, silu_banks = {}, {}, {}
        w_rows, w_banks, w_grouped = {}, {}, {}
        flat, flat_codes, flat_scales = {}, {}, {}
        sums, base_sums, rows_out, passes_done = {}, {}, {}, {}

        def bank(name):
            return bank_pool.tile([P, 2, 256], F32, name=name, tag="bank")

        def flat_tile(mu):
            if mu not in flat:
                flat[mu] = flat_pool.tile([P, ORDERS, P, 4], BF16, name="flat%d" % mu, tag="flat", align_bytes=64)
            return flat[mu]

        def load_x(k):
            x_rows[k] = x_pool.tile([P, 2, IN], BF16, name="x_rows%d" % k, tag="x_rows")
            nc.sync.dma_start(out=x_rows[k][:], in_=x[256 * k:256 * k + 256, :].rearrange("(a p) i -> p a i", p=P))

        def load_w(g):
            w_rows[g] = w_pool.tile([P, 4, 1024], BF16, name="w_rows%d" % g, tag="w_rows")
            nc.sync.dma_start(out=w_rows[g][:],
                              in_=w_flat[:, 1024 * g:1024 * g + 1024].rearrange("(h p) j -> p h j", p=P))

        def load_base_weight():
            nc.sync.dma_start(out=base_codes[:].bitcast(I32),
                              in_=base_weight_words[0].rearrange("p n t -> p (n t)").bitcast(I32))
            for quadrant in range(4):
                nc.sync.dma_start(out=base_scales[32 * quadrant:32 * quadrant + 4, :].bitcast(I32),
                                  in_=base_weight_scales[0, 4 * quadrant:4 * quadrant + 4, :].bitcast(I32))

        def transpose_x(k):
            x_banks[k] = bank("x_bank%d" % k)
            for a in range(2):
                words = x_rows[k][:, a, :].bitcast(F32)
                for u in range(2):
                    nc.tensor.transpose(x_banks[k][:, u, P * a:P * a + P], words[:, P * u:P * u + P], identity[:])

        def sort_x(k):
            first = 256 * k
            q_lo, q_hi = -(-first // 10), (first + 256) // 10
            head, tail = 10 * q_lo - first, first + 256 - 10 * q_hi
            nc.vector.tensor_copy(
                out=xs_words[:, :, q_lo:q_hi, :],
                in_=x_banks[k][:, :, head:head + 10 * (q_hi - q_lo)].rearrange("p u (q r) -> p r q u", r=10))
            if head:
                nc.vector.tensor_copy(out=xs_words[:, 10 - head:10, q_lo - 1, :],
                                      in_=x_banks[k][:, :, 0:head].rearrange("p u r -> p r u"))
            if tail:
                nc.vector.tensor_copy(out=xs_words[:, 0:tail, q_hi, :],
                                      in_=x_banks[k][:, :, 256 - tail:256].rearrange("p u r -> p r u"))

        def transpose_x_for_silu(k):
            silu_banks[k] = bank("silu_bank%d" % k)
            for a in range(2):
                words = x_rows[k][:, a, :].bitcast(F32)
                for u in range(2):
                    nc.tensor.transpose(silu_banks[k][:, u, P * a:P * a + P], words[:, u:256:2], identity[:])

        def silu(k):
            nc.scalar.activation(out=silu_bf[:, 256 * k:256 * k + 256, :, :],
                                 in_=silu_banks[k][:].bitcast(BF16).rearrange("p u (b e) -> p b u e", e=2),
                                 func=ACT.Silu)

        def quantise_silu():
            nc.vector.quantize_mx(out=silu_codes[:].bitcast(FP8X4), scales=silu_scales[:],
                                  in_=silu_bf[:].rearrange("p b u e -> p (b u e)"))

        def transpose_w(g):
            for h in range(4):
                w_banks[g, h] = bank("w_bank%d_%d" % (g, h))
                for a in range(2):
                    words = w_rows[g][:, 2 * (h % 2) + a, :].bitcast(F32)
                    for u in range(2):
                        low = 256 * (h // 2) + P * u
                        nc.tensor.transpose(w_banks[g, h][:, u, P * a:P * a + P], words[:, low:low + P], identity[:])

        def group_w(g):
            w_grouped[g] = wg_pool.tile([P, 2, OUT, 4], BF16, name="w_grouped%d" % g, tag="w_grouped", align_bytes=64)
            for h in range(4):
                nc.scalar.copy(out=w_grouped[g][:].bitcast(F32)[:, h // 2, 256 * (h % 2):256 * (h % 2) + 256, :],
                               in_=w_banks[g, h][:].rearrange("p u o -> p o u"))

        def quantise_w(g):
            nc.vector.quantize_mx(out=w_codes[:, 2 * g:2 * g + 2, :].rearrange("p c o -> p (c o)").bitcast(FP8X4),
                                  scales=w_scales[:, 2 * g:2 * g + 2, :].rearrange("p c o -> p (c o)"),
                                  in_=w_grouped[g][:].rearrange("p c o t -> p (c o t)"))

        def square(dst, src, scale, bias, slots):
            nc.scalar.activation(out=dst[:, :, slots[0]:slots[1], :], in_=src[:, :, slots[0]:slots[1], :],
                                 func=ACT.Square, bias=bias, scale=scale)

        def shifted_product(dst, in0, shift, in1, slots):
            nc.vector.scalar_tensor_tensor(out=dst[:, :, slots[0]:slots[1], :], in0=in0[:, :, slots[0]:slots[1], :],
                                           scalar=shift, in1=in1[:, :, slots[0]:slots[1], :],
                                           op0=ALU.add, op1=ALU.mult)

        def place(n, emit, tiles=None, cut=None):
            for mu, q, count, column, rho, c, classes in runs_of_order(n, cut):
                if tiles is None or mu in tiles:
                    emit(flat_tile(mu)[:, c:c + classes, column:column + count, :],
                         lambda t: t[:, rho:rho + classes, q:q + count, :])

        def copy_of(src):
            return lambda dst, part: nc.vector.tensor_copy(out=dst, in_=part(src))

        def half_minus_one(src):
            return lambda dst, part: nc.vector.tensor_scalar(out=dst, in0=part(src), scalar1=0.5, scalar2=-1.0,
                                                             op0=ALU.mult, op1=ALU.add)

        def half_minus_one_on_scalar(src):
            return lambda dst, part: nc.scalar.activation(out=dst, in_=part(src), func=ACT.Copy, bias=-1.0, scale=0.5)

        def product_of(in0, shift, in1):
            return lambda dst, part: nc.vector.scalar_tensor_tensor(out=dst, in0=part(in0), scalar=shift, in1=part(in1),
                                                                    op0=ALU.add, op1=ALU.mult)

        def difference_of(in0, in1):
            return lambda dst, part: nc.vector.tensor_tensor(out=dst, in0=part(in0), in1=part(in1), op=ALU.subtract)

        def quantise_flat(mu, pieces=((0, 8), (8, 2))):
            if mu not in flat_codes:
                flat_codes[mu] = code_pool.tile([P, ORDERS * P], U32, name="flat_codes%d" % mu, tag="codes", align_bytes=64)
                flat_scales[mu] = code_pool.tile([P, ORDERS * P], U8, name="flat_scales%d" % mu, tag="scales",
                                                 align_bytes=64)
            for c, count in pieces:
                nc.vector.quantize_mx(out=flat_codes[mu][:, P * c:P * (c + count)].bitcast(FP8X4),
                                      scales=flat_scales[mu][:, P * c:P * (c + count)],
                                      in_=flat[mu][:, c:c + count, :, :].rearrange("p c m t -> p (c m t)"))

        def spline_passes(mu, first=0, count=ORDERS):
            if mu not in sums:
                sums[mu] = bank("sum%d" % mu)
            for c in range(first, first + count):
                passes_done[mu] = passes_done.get(mu, 0) + 1
                nc.tensor.matmul_mx(out=sums[mu][:].rearrange("p a b -> p (a b)"),
                                    lhsT=flat_codes[mu][:, P * c:P * c + P].bitcast(FP8X4),
                                    lhsT_scale=flat_scales[mu][:, P * c:P * c + P],
                                    rhs=w_codes[:, c, :].bitcast(FP8X4), rhs_scale=w_scales[:, c, :],
                                    start=(passes_done[mu] == 1), stop=(passes_done[mu] == ORDERS))

        def base_pass(mu):
            base_sums[mu] = base_pool.tile([P, OUT], F32, name="base_sum%d" % mu, tag="base_sum")
            nc.tensor.matmul_mx(out=base_sums[mu][:], lhsT=silu_codes[:, P * mu:P * mu + P].bitcast(FP8X4),
                                lhsT_scale=silu_scales[:, P * mu:P * mu + P],
                                rhs=base_codes[:].bitcast(FP8X4), rhs_scale=base_scales[:], start=True, stop=True)

        def base_out(mu):
            rows_out[mu] = out_pool.tile([P, OUT], F32, name="rows_out%d" % mu, tag="rows_out")
            nc.scalar.copy(out=rows_out[mu][:], in_=base_sums[mu][:])

        def finish(mu):
            nc.vector.scalar_tensor_tensor(out=rows_out[mu][:], in0=sums[mu][:].rearrange("p a b -> p (a b)"), scalar=0.1,
                                           in1=rows_out[mu][:], op0=ALU.mult, op1=ALU.add)
            nc.sync.dma_start(out=out[P * mu:P * mu + P, :], in_=rows_out[mu][:])

        make_identity(nc, identity[:])
        nc.vector.memset(xs_words[:, :, 102:SLOTS, :], 0.0)
        nc.vector.memset(base_scales[:].bitcast(I32), 0)
        nc.vector.memset(flat_tile(0)[:], 1.0)
        for k in range(4):
            load_x(k)
        for g in range(3):
            load_w(g)

        for k in range(4):
            transpose_x(k)
            sort_x(k)
        for slots in QUARTERS:
            square(buf_y, xs, 2.0, 0.0, slots)
        place(1, copy_of(xs))
        quantise_flat(0)
        for slots in HALVES:
            shifted_product(buf_3, buf_y, -3.0, xs, slots)

        for g in range(5):
            transpose_w(g)
            if g + 3 < 5:
                load_w(g + 3)
            if g == 1:
                load_base_weight()
            group_w(g)
            quantise_w(g)
            if g == 0:
                place(2, half_minus_one(buf_y))
            elif g == 1:
                quantise_flat(1)
            elif g == 2:
                square(buf_4, buf_y, 1.0, -2.0, HALVES[0])
                place(3, copy_of(buf_3))
            elif g == 3:
                square(buf_4, buf_y, 1.0, -2.0, HALVES[1])
                quantise_flat(2)
                place(4, half_minus_one(buf_4))
            else:
                quantise_flat(3)

        for k in range(4):
            transpose_x_for_silu(k)
        for mu in range(4):
            spline_passes(mu)

        for slots in HALVES:
            square(buf_y, buf_y, 1.0, -2.5, slots)
        for slots in HALVES:
            square(buf_6, buf_3, 2.0, 0.0, slots)
        for k in range(4):
            silu(k)
        place(5, product_of(buf_y, -1.25, xs), cut=HALVES[0][1])
        shifted_product(buf_y, buf_4, -2.0, buf_3, HALVES[0])
        place(6, half_minus_one_on_scalar(buf_6), tiles=(4,))
        place(6, half_minus_one(buf_6), tiles=(5,))
        shifted_product(buf_y, buf_4, -2.0, buf_3, HALVES[1])
        for slots in HALVES:
            square(buf_4, buf_4, 1.0, -2.0, slots)
        place(7, difference_of(buf_y, xs), tiles=(5,))
        quantise_silu()
        base_pass(0)
        base_pass(1)
        quantise_flat(4)
        spline_passes(4)
        base_pass(2)
        base_pass(3)
        quantise_flat(5)
        spline_passes(5)
        base_pass(4)
        base_pass(5)
        place(7, difference_of(buf_y, xs), tiles=(6,))
        place(8, half_minus_one_on_scalar(buf_4), tiles=(7,))
        base_out(0)
        base_out(1)
        place(8, half_minus_one_on_scalar(buf_4), tiles=(6,))

        ninth = runs_of_order(9)
        place_ninth = product_of(buf_6, -3.0, buf_3)

        def place_run(run):
            mu, q, count, column, rho, c, classes = run
            place_ninth(flat_tile(mu)[:, c:c + classes, column:column + count, :],
                        lambda t: t[:, rho:rho + classes, q:q + count, :])

        place_run(ninth[0])
        finish(0)
        finish(1)
        quantise_flat(6)
        spline_passes(6)
        quantise_flat(7, ((0, 4), (4, 2)))
        spline_passes(7, 0, 6)
        base_pass(6)
        base_pass(7)
        for mu in range(2, TILES):
            base_out(mu)
        place_run(ninth[1])
        finish(2)
        finish(3)
        quantise_flat(7, ((6, 4),))
        spline_passes(7, 6, 4)
        for mu in range(4, TILES):
            finish(mu)
